import numpy as np
import ml_dtypes


def mxq(x, axis, fmt="e4m3"):
    dtype, down = {"e4m3": (ml_dtypes.float8_e4m3fn, 7), "e5m2": (ml_dtypes.float8_e5m2, 14)}[fmt]
    v = np.moveaxis(np.asarray(x, np.float32).astype(ml_dtypes.bfloat16).astype(np.float64), axis, -1)
    blocks = v.reshape(v.shape[:-1] + (-1, 32))
    amax = np.abs(blocks).max(-1, keepdims=True)
    byte = np.maximum(np.where(amax > 0, np.frexp(amax)[1] - 1 + 127, 0) - down, 1)
    scale = np.exp2(byte - 127.0)
    codes = (blocks / scale).astype(np.float32).astype(dtype).astype(np.float64)
    return np.moveaxis((codes * scale).reshape(v.shape), -1, axis)


WIDE = False


def mx_kscale(k):
    if not WIDE:
        return np.ones(k)
    levels = np.array([10, -10, 5, -5, 0])
    a = np.random.permutation(np.resize(levels, k // 512 * 4)).reshape(k // 512, 4)
    idx = np.arange(k)
    return np.exp2(a[idx // 512, idx % 128 // 32])


BF16 = ml_dtypes.bfloat16


def bf(x):
    return np.asarray(x, np.float32).astype(BF16)


def f64(x):
    return np.asarray(x).astype(np.float64)


N, C, F, O, DEG = 2048, 512, 512, 40, 16


def draw_adj():
    hit = (np.random.random((N, N)) < 0.5 * DEG / N).astype(np.float64)
    wt = 0.5 + np.random.random((N, N))
    return np.clip(hit + hit.T + np.eye(N), 0.0, 1.0) * (wt + wt.T) * 0.5


def setup_inputs():
    t = mx_kscale(C)
    return {"x": bf(np.random.standard_normal((N, C)) * t),
            "adj": bf(draw_adj()),
            "alpha": bf(0.5 + 0.1 * np.random.standard_normal(1)),
            "rezero_w": bf(np.random.standard_normal((C, C)) * np.sqrt(DEG) / np.sqrt(C) / t[:, None] * t[None, :])}


def reference(x, adj, alpha, rezero_w):
    x, adj = f64(x), f64(adj)
    deg = np.sum(adj, axis=1)
    dis = deg ** -0.5
    norm_adj = dis[:, None] * adj * dis[None, :]
    agg = mxq(norm_adj, 1, "e4m3") @ mxq(x, 0, "e4m3")
    return x + f64(alpha) * (mxq(agg, 1, "e4m3") @ mxq(f64(rezero_w), 0, "e4m3"))

@@ -1,0 +1,230 @@
+from contextlib import ExitStack
+
+import concourse.mybir as mybir
+from concourse.masks import make_identity
+
+BF16 = mybir.dt.bfloat16
+F32 = mybir.dt.float32
+U32 = mybir.dt.uint32
+U8 = mybir.dt.uint8
+FP8X4 = mybir.dt.float8_e4m3fn_x4
+MULT = mybir.AluOpType.mult
+ADD = mybir.AluOpType.add
+SQRT = mybir.ActivationFunctionType.Sqrt
+
+P = 128
+PACK = 4
+GROUP = P * PACK
+NODES = 2048
+FEATURES = 512
+GROUPS = NODES // GROUP
+ONES_WIDTH = 32
+
+FLOPS = 2 * NODES * NODES * FEATURES + 2 * NODES * FEATURES * FEATURES
+
+
+def regroup(engine_copy, grouped, planes):
+    engine_copy(
+        out=grouped.rearrange("p (c i) t -> p c t i", i=4),
+        in_=planes.rearrange("p t (c i) -> p c t i", i=4),
+    )
+
+
+def quantise(nc, grouped, codes, scales):
+    nc.vector.quantize_mx(
+        out=codes.bitcast(FP8X4),
+        scales=scales,
+        in_=grouped.rearrange("p c t -> p (c t)"),
+    )
+
+
+def tile_sage_re_pa_kernel(tc, x, adj, alpha, rezero_w, out):
+    nc = tc.nc
+    with ExitStack() as pools:
+        keep = pools.enter_context(tc.tile_pool(name="keep", bufs=1))
+        stage = pools.enter_context(tc.tile_pool(name="stage", bufs=3))
+        rows_pool = pools.enter_context(tc.tile_pool(name="rows_pool", bufs=6))
+        psum_row = pools.enter_context(tc.psum_pool(name="psum_row", bufs=3))
+        psum_plain = pools.enter_context(tc.psum_pool(name="psum_plain", bufs=2))
+        psum_agg = pools.enter_context(tc.psum_pool(name="psum_agg", bufs=2))
+        psum_out = pools.enter_context(tc.psum_pool(name="psum_out", bufs=1))
+
+        adj_cols = []
+        for s in range(GROUPS):
+            adj_view = adj[:, s * GROUP : (s + 1) * GROUP].rearrange("(a p) f -> p a f", p=P)
+            pieces = []
+            for q in range(GROUPS):
+                piece = keep.tile([P, PACK, GROUP], BF16, name="adj_%d_%d" % (q, s))
+                nc.sync.dma_start(out=piece[:], in_=adj_view[:, q * PACK : (q + 1) * PACK, :])
+                pieces.append(piece)
+            adj_cols.append(pieces)
+        x_view = x.rearrange("(a p) c -> p a c", p=P)
+        x_rows = []
+        for h in range(GROUPS):
+            x_h = keep.tile([P, PACK, FEATURES], BF16, name="x_rows%d" % h)
+            nc.sync.dma_start(out=x_h[:], in_=x_view[:, h * PACK : (h + 1) * PACK, :])
+            x_rows.append(x_h)
+        w_rows = keep.tile([P, PACK, FEATURES], BF16)
+        nc.sync.dma_start(out=w_rows[:], in_=rezero_w.rearrange("(t p) n -> p t n", p=P))
+        alpha_bf = keep.tile([P, 1], BF16)
+        nc.scalar.dma_start(out=alpha_bf[:], in_=alpha.partition_broadcast(P))
+
+        ones = keep.tile([P, ONES_WIDTH], BF16)
+        nc.vector.memset(ones[:], 1.0)
+        ident_bf = keep.tile([P, P], BF16)
+        make_identity(nc, ident_bf[:])
+        ident_f32 = keep.tile([P, P], F32)
+        make_identity(nc, ident_f32[:])
+        alpha_f32 = keep.tile([P, 1], F32)
+        nc.vector.tensor_copy(out=alpha_f32[:], in_=alpha_bf[:])
+        warm = keep.tile([P, 1], F32)
+        nc.scalar.activation(out=warm[:], in_=ones[:, 0:1], func=SQRT)
+
+        dis_col = []
+        dis_row = []
+        for s in range(GROUPS):
+            part = psum_plain.tile([P, GROUPS, PACK, ONES_WIDTH], F32, tag="plain")
+            for q in range(GROUPS):
+                for b in range(PACK):
+                    for t in range(PACK):
+                        nc.tensor.matmul(
+                            out=part[:, q, b, :],
+                            lhsT=adj_cols[s][q][:, t, b * P : (b + 1) * P],
+                            rhs=ones[:],
+                            start=(t == 0),
+                            stop=(t == PACK - 1),
+                        )
+            deg = stage.tile([P, PACK], F32)
+            nc.vector.tensor_reduce(
+                out=deg[:],
+                in_=part[:, :, :, 0].rearrange("p q b -> p b q"),
+                axis=mybir.AxisListType.X,
+                op=ADD,
+            )
+            inverse = stage.tile([P, PACK], F32)
+            nc.vector.reciprocal(out=inverse[:], in_=deg[:])
+            col_s = keep.tile([P, PACK], F32, name="dis_col%d" % s)
+            nc.scalar.activation(out=col_s[:], in_=inverse[:], func=SQRT)
+            dis_col.append(col_s)
+            row_s = psum_row.tile([P, GROUP], F32, tag="row")
+            for b in range(PACK):
+                nc.tensor.transpose(
+                    out=row_s[:, b * P : (b + 1) * P],
+                    in_=col_s[:, b : b + 1].to_broadcast([P, P]),
+                    identity=ident_f32[:],
+                )
+            dis_row.append(row_s)
+
+        x_codes = []
+        x_scales = []
+        for h in range(GROUPS):
+            x_grouped = stage.tile([P, FEATURES, PACK], BF16, align_bytes=64)
+            regroup(nc.scalar.copy, x_grouped, x_rows[h])
+            x_codes.append(keep.tile([P, FEATURES], U32, name="x_codes%d" % h, align_bytes=64))
+            x_scales.append(keep.tile([P, FEATURES], U8, name="x_scales%d" % h, align_bytes=64))
+            quantise(nc, x_grouped, x_codes[h][:], x_scales[h][:])
+        w_codes = keep.tile([P, FEATURES], U32, align_bytes=64)
+        w_scales = keep.tile([P, FEATURES], U8, align_bytes=64)
+        w_grouped = keep.tile([P, FEATURES, PACK], BF16, align_bytes=64)
+        regroup(nc.scalar.copy, w_grouped, w_rows)
+        quantise(nc, w_grouped, w_codes[:], w_scales[:])
+
+        n_codes = {}
+        n_scales = {}
+        for h in range(GROUPS):
+            for r in range(GROUPS):
+                n_codes[h, r] = keep.tile(
+                    [P, GROUP], U32, name="n_codes_%d_%d" % (h, r), align_bytes=64
+                )
+                n_scales[h, r] = keep.tile(
+                    [P, GROUP], U8, name="n_scales_%d_%d" % (h, r), align_bytes=64
+                )
+
+        def normalise_square(g, s):
+            square = stage.tile([P, PACK, GROUP], BF16)
+            for t in range(PACK):
+                nc.vector.scalar_tensor_tensor(
+                    out=square[:, t, :],
+                    in0=adj_cols[s][g][:, t, :],
+                    scalar=dis_col[g][:, t : t + 1],
+                    in1=dis_row[s][:],
+                    op0=MULT,
+                    op1=MULT,
+                )
+            direct = stage.tile([P, GROUP, PACK], BF16, align_bytes=64)
+            nc.gpsimd.tensor_scalar(
+                out=direct[:],
+                in0=square.rearrange("p t f -> p f t"),
+                scalar1=1.0,
+                scalar2=0.0,
+                op0=MULT,
+                op1=ADD,
+            )
+            quantise(nc, direct, n_codes[g, s][:], n_scales[g, s][:])
+            if g == s:
+                return
+            mirrored = stage.tile([P, GROUP, PACK], BF16, align_bytes=64)
+            for half in range(2):
+                flipped = psum_plain.tile([P, 2, PACK, P], BF16, tag="plain")
+                for u in range(2):
+                    for tj in range(PACK):
+                        nc.tensor.transpose(
+                            out=flipped[:, u, tj, :],
+                            in_=square[:, 2 * half + u, tj * P : (tj + 1) * P],
+                            identity=ident_bf[:],
+                        )
+                nc.scalar.copy(
+                    out=mirrored[:, 2 * half * P : 2 * (half + 1) * P, :].rearrange(
+                        "p (u m) t -> p u m t", u=2
+                    ),
+                    in_=flipped.rearrange("p u t m -> p u m t"),
+                )
+            quantise(nc, mirrored, n_codes[s, g][:], n_scales[s, g][:])
+
+        def finish_rows(r, b):
+            first = r * GROUP + b * P
+            cols = slice(b * P, (b + 1) * P)
+            agg_t = psum_agg.tile([P, PACK, P], F32)
+            for t in range(PACK):
+                for h in range(GROUPS):
+                    nc.tensor.matmul_mx(
+                        out=agg_t[:, t, :],
+                        lhsT=x_codes[h][:, t * P : (t + 1) * P].bitcast(FP8X4),
+                        lhsT_scale=x_scales[h][:, t * P : (t + 1) * P],
+                        rhs=n_codes[h, r][:, cols].bitcast(FP8X4),
+                        rhs_scale=n_scales[h, r][:, cols],
+                        start=(h == 0),
+                        stop=(h == GROUPS - 1),
+                    )
+            agg_grouped = rows_pool.tile([P, P, PACK], BF16, align_bytes=64)
+            nc.scalar.copy(out=agg_grouped[:], in_=agg_t.rearrange("p t m -> p m t"))
+            agg_codes = rows_pool.tile([P, P], U32, align_bytes=64)
+            agg_scales = rows_pool.tile([P, P], U8, align_bytes=64)
+            quantise(nc, agg_grouped, agg_codes[:], agg_scales[:])
+            product = psum_out.tile([P, FEATURES], F32)
+            nc.tensor.matmul_mx(
+                out=product[:],
+                lhsT=agg_codes[:].bitcast(FP8X4),
+                lhsT_scale=agg_scales[:],
+                rhs=w_codes[:].bitcast(FP8X4),
+                rhs_scale=w_scales[:],
+                start=True,
+                stop=True,
+            )
+            result = rows_pool.tile([P, FEATURES], F32)
+            nc.vector.scalar_tensor_tensor(
+                out=result[:],
+                in0=product[:],
+                scalar=alpha_f32[:, 0:1],
+                in1=x_rows[r][:, b, :],
+                op0=MULT,
+                op1=ADD,
+            )
+            nc.sync.dma_start(out=out[first : first + P, :], in_=result[:])
+
+        for g in range(GROUPS):
+            for s in range(g, GROUPS):
+                normalise_square(g, s)
+        for r in range(GROUPS):
+            for b in range(PACK):
+                finish_rows(r, b)

@@ -42,12 +42,13 @@ def tile_sage_re_pa_kernel(tc, x, adj, alpha, rezero_w, out):
     nc = tc.nc
     with ExitStack() as pools:
         keep = pools.enter_context(tc.tile_pool(name="keep", bufs=1))
-        stage = pools.enter_context(tc.tile_pool(name="stage", bufs=3))
+        stage = pools.enter_context(tc.tile_pool(name="stage", bufs=4))
+        x_stage = pools.enter_context(tc.tile_pool(name="x_stage", bufs=2))
         rows_pool = pools.enter_context(tc.tile_pool(name="rows_pool", bufs=6))
-        psum_row = pools.enter_context(tc.psum_pool(name="psum_row", bufs=3))
+        psum_row = pools.enter_context(tc.psum_pool(name="psum_row", bufs=2))
         psum_plain = pools.enter_context(tc.psum_pool(name="psum_plain", bufs=2))
         psum_agg = pools.enter_context(tc.psum_pool(name="psum_agg", bufs=2))
-        psum_out = pools.enter_context(tc.psum_pool(name="psum_out", bufs=1))
+        psum_out = pools.enter_context(tc.psum_pool(name="psum_out", bufs=2))
 
         adj_cols = []
         for s in range(GROUPS):
@@ -118,7 +119,7 @@ def tile_sage_re_pa_kernel(tc, x, adj, alpha, rezero_w, out):
         x_codes = []
         x_scales = []
         for h in range(GROUPS):
-            x_grouped = stage.tile([P, FEATURES, PACK], BF16, align_bytes=64)
+            x_grouped = x_stage.tile([P, FEATURES, PACK], BF16, align_bytes=64)
             regroup(nc.scalar.copy, x_grouped, x_rows[h])
             x_codes.append(keep.tile([P, FEATURES], U32, name="x_codes%d" % h, align_bytes=64))
             x_scales.append(keep.tile([P, FEATURES], U8, name="x_scales%d" % h, align_bytes=64))
@@ -152,14 +153,7 @@ def tile_sage_re_pa_kernel(tc, x, adj, alpha, rezero_w, out):
                     op1=MULT,
                 )
             direct = stage.tile([P, GROUP, PACK], BF16, align_bytes=64)
-            nc.gpsimd.tensor_scalar(
-                out=direct[:],
-                in0=square.rearrange("p t f -> p f t"),
-                scalar1=1.0,
-                scalar2=0.0,
-                op0=MULT,
-                op1=ADD,
-            )
+            regroup(nc.scalar.copy if g == s else nc.vector.tensor_copy, direct, square)
             quantise(nc, direct, n_codes[g, s][:], n_scales[g, s][:])
             if g == s:
                 return
@@ -222,8 +216,9 @@ def tile_sage_re_pa_kernel(tc, x, adj, alpha, rezero_w, out):
             )
             nc.sync.dma_start(out=out[first : first + P, :], in_=result[:])
 
-        for g in range(GROUPS):
-            for s in range(g, GROUPS):
+        for diagonal in range(2 * GROUPS - 1):
+            for g in range(max(0, diagonal - GROUPS + 1), diagonal // 2 + 1):
+                s = diagonal - g
                 normalise_square(g, s)
         for r in range(GROUPS):
             for b in range(PACK):

@@ -19,6 +19,7 @@ NODES = 2048
 FEATURES = 512
 GROUPS = NODES // GROUP
 ONES_WIDTH = 32
+AHEAD = 3
 
 FLOPS = 2 * NODES * NODES * FEATURES + 2 * NODES * FEATURES * FEATURES
 
@@ -27,6 +28,17 @@ def regroup(engine_copy, grouped, planes):
     engine_copy(
         out=grouped.rearrange("p (c i) t -> p c t i", i=4),
         in_=planes.rearrange("p t (c i) -> p c t i", i=4),
+    )
+
+
+def regroup_on_gpsimd(nc, grouped, planes):
+    nc.gpsimd.tensor_scalar(
+        out=grouped[:],
+        in0=planes.rearrange("p t c -> p c t"),
+        scalar1=1.0,
+        scalar2=0.0,
+        op0=MULT,
+        op1=ADD,
     )
 
 
@@ -42,13 +54,12 @@ def tile_sage_re_pa_kernel(tc, x, adj, alpha, rezero_w, out):
     nc = tc.nc
     with ExitStack() as pools:
         keep = pools.enter_context(tc.tile_pool(name="keep", bufs=1))
-        stage = pools.enter_context(tc.tile_pool(name="stage", bufs=4))
+        stage = pools.enter_context(tc.tile_pool(name="stage", bufs=3))
         x_stage = pools.enter_context(tc.tile_pool(name="x_stage", bufs=2))
         rows_pool = pools.enter_context(tc.tile_pool(name="rows_pool", bufs=6))
-        psum_row = pools.enter_context(tc.psum_pool(name="psum_row", bufs=2))
-        psum_plain = pools.enter_context(tc.psum_pool(name="psum_plain", bufs=2))
-        psum_agg = pools.enter_context(tc.psum_pool(name="psum_agg", bufs=2))
-        psum_out = pools.enter_context(tc.psum_pool(name="psum_out", bufs=2))
+        agg_pool = pools.enter_context(tc.tile_pool(name="agg_pool", bufs=1))
+        psum_wide = pools.enter_context(tc.psum_pool(name="psum_wide", bufs=4))
+        psum_work = pools.enter_context(tc.psum_pool(name="psum_work", bufs=4))
 
         adj_cols = []
         for s in range(GROUPS):
@@ -84,7 +95,7 @@ def tile_sage_re_pa_kernel(tc, x, adj, alpha, rezero_w, out):
         dis_col = []
         dis_row = []
         for s in range(GROUPS):
-            part = psum_plain.tile([P, GROUPS, PACK, ONES_WIDTH], F32, tag="plain")
+            part = psum_work.tile([P, GROUPS, PACK, ONES_WIDTH], F32, tag="work")
             for q in range(GROUPS):
                 for b in range(PACK):
                     for t in range(PACK):
@@ -107,7 +118,7 @@ def tile_sage_re_pa_kernel(tc, x, adj, alpha, rezero_w, out):
             col_s = keep.tile([P, PACK], F32, name="dis_col%d" % s)
             nc.scalar.activation(out=col_s[:], in_=inverse[:], func=SQRT)
             dis_col.append(col_s)
-            row_s = psum_row.tile([P, GROUP], F32, tag="row")
+            row_s = psum_wide.tile([P, GROUP], F32, tag="wide")
             for b in range(PACK):
                 nc.tensor.transpose(
                     out=row_s[:, b * P : (b + 1) * P],
@@ -120,14 +131,14 @@ def tile_sage_re_pa_kernel(tc, x, adj, alpha, rezero_w, out):
         x_scales = []
         for h in range(GROUPS):
             x_grouped = x_stage.tile([P, FEATURES, PACK], BF16, align_bytes=64)
-            regroup(nc.scalar.copy, x_grouped, x_rows[h])
+            regroup_on_gpsimd(nc, x_grouped, x_rows[h])
             x_codes.append(keep.tile([P, FEATURES], U32, name="x_codes%d" % h, align_bytes=64))
             x_scales.append(keep.tile([P, FEATURES], U8, name="x_scales%d" % h, align_bytes=64))
             quantise(nc, x_grouped, x_codes[h][:], x_scales[h][:])
         w_codes = keep.tile([P, FEATURES], U32, align_bytes=64)
         w_scales = keep.tile([P, FEATURES], U8, align_bytes=64)
         w_grouped = keep.tile([P, FEATURES, PACK], BF16, align_bytes=64)
-        regroup(nc.scalar.copy, w_grouped, w_rows)
+        regroup_on_gpsimd(nc, w_grouped, w_rows)
         quantise(nc, w_grouped, w_codes[:], w_scales[:])
 
         n_codes = {}
@@ -153,13 +164,12 @@ def tile_sage_re_pa_kernel(tc, x, adj, alpha, rezero_w, out):
                     op1=MULT,
                 )
             direct = stage.tile([P, GROUP, PACK], BF16, align_bytes=64)
-            regroup(nc.scalar.copy if g == s else nc.vector.tensor_copy, direct, square)
-            quantise(nc, direct, n_codes[g, s][:], n_scales[g, s][:])
+            regroup(nc.scalar.copy, direct, square)
             if g == s:
-                return
+                return direct, None
             mirrored = stage.tile([P, GROUP, PACK], BF16, align_bytes=64)
             for half in range(2):
-                flipped = psum_plain.tile([P, 2, PACK, P], BF16, tag="plain")
+                flipped = psum_work.tile([P, 2, PACK, P], BF16, tag="work")
                 for u in range(2):
                     for tj in range(PACK):
                         nc.tensor.transpose(
@@ -173,12 +183,18 @@ def tile_sage_re_pa_kernel(tc, x, adj, alpha, rezero_w, out):
                     ),
                     in_=flipped.rearrange("p u t m -> p u m t"),
                 )
-            quantise(nc, mirrored, n_codes[s, g][:], n_scales[s, g][:])
+            return direct, mirrored
 
-        def finish_rows(r, b):
-            first = r * GROUP + b * P
+        def quantise_square(g, s, direct, mirrored):
+            quantise(nc, direct, n_codes[g, s][:], n_scales[g, s][:])
+            if mirrored is not None:
+                quantise(nc, mirrored, n_codes[s, g][:], n_scales[s, g][:])
+
+        agg_grouped = {}
+
+        def aggregate_rows(r, b):
             cols = slice(b * P, (b + 1) * P)
-            agg_t = psum_agg.tile([P, PACK, P], F32)
+            agg_t = psum_work.tile([P, PACK, P], F32, tag="work")
             for t in range(PACK):
                 for h in range(GROUPS):
                     nc.tensor.matmul_mx(
@@ -190,12 +206,18 @@ def tile_sage_re_pa_kernel(tc, x, adj, alpha, rezero_w, out):
                         start=(h == 0),
                         stop=(h == GROUPS - 1),
                     )
-            agg_grouped = rows_pool.tile([P, P, PACK], BF16, align_bytes=64)
-            nc.scalar.copy(out=agg_grouped[:], in_=agg_t.rearrange("p t m -> p m t"))
+            agg_grouped[r, b] = agg_pool.tile(
+                [P, P, PACK], BF16, name="agg_grouped_%d_%d" % (r, b), align_bytes=64
+            )
+            nc.scalar.copy(out=agg_grouped[r, b][:], in_=agg_t.rearrange("p t m -> p m t"))
+
+        products = {}
+
+        def second_matmul(r, b):
             agg_codes = rows_pool.tile([P, P], U32, align_bytes=64)
             agg_scales = rows_pool.tile([P, P], U8, align_bytes=64)
-            quantise(nc, agg_grouped, agg_codes[:], agg_scales[:])
-            product = psum_out.tile([P, FEATURES], F32)
+            quantise(nc, agg_grouped[r, b], agg_codes[:], agg_scales[:])
+            product = psum_wide.tile([P, FEATURES], F32, tag="wide")
             nc.tensor.matmul_mx(
                 out=product[:],
                 lhsT=agg_codes[:].bitcast(FP8X4),
@@ -205,10 +227,14 @@ def tile_sage_re_pa_kernel(tc, x, adj, alpha, rezero_w, out):
                 start=True,
                 stop=True,
             )
+            products[r, b] = product
+
+        def add_residual(r, b):
+            first = r * GROUP + b * P
             result = rows_pool.tile([P, FEATURES], F32)
             nc.vector.scalar_tensor_tensor(
                 out=result[:],
-                in0=product[:],
+                in0=products[r, b][:],
                 scalar=alpha_f32[:, 0:1],
                 in1=x_rows[r][:, b, :],
                 op0=MULT,
@@ -216,10 +242,26 @@ def tile_sage_re_pa_kernel(tc, x, adj, alpha, rezero_w, out):
             )
             nc.sync.dma_start(out=out[first : first + P, :], in_=result[:])
 
-        for diagonal in range(2 * GROUPS - 1):
-            for g in range(max(0, diagonal - GROUPS + 1), diagonal // 2 + 1):
-                s = diagonal - g
-                normalise_square(g, s)
-        for r in range(GROUPS):
-            for b in range(PACK):
-                finish_rows(r, b)
+        squares = [
+            (g, diagonal - g)
+            for diagonal in range(2 * GROUPS - 1)
+            for g in range(max(0, diagonal - GROUPS + 1), diagonal // 2 + 1)
+        ]
+        grouped = {}
+        for n in range(len(squares) + 1):
+            if n < len(squares):
+                grouped[n] = normalise_square(*squares[n])
+            if n > 0:
+                g, s = squares[n - 1]
+                quantise_square(g, s, *grouped[n - 1])
+                if s == GROUPS - 1:
+                    for b in range(PACK):
+                        aggregate_rows(g, b)
+
+        blocks = [(r, b) for r in range(GROUPS) for b in range(PACK)]
+        with tc.manual_schedule():
+            for k in range(len(blocks) + AHEAD):
+                if k < len(blocks):
+                    second_matmul(*blocks[k])
+                if k >= AHEAD:
+                    add_residual(*blocks[k - AHEAD])

@@ -19,6 +19,7 @@ NODES = 2048
 FEATURES = 512
 GROUPS = NODES // GROUP
 ONES_WIDTH = 32
+GROUPS_BEFORE_X = 2
 AHEAD = 3
 
 FLOPS = 2 * NODES * NODES * FEATURES + 2 * NODES * FEATURES * FEATURES
@@ -28,17 +29,6 @@ def regroup(engine_copy, grouped, planes):
     engine_copy(
         out=grouped.rearrange("p (c i) t -> p c t i", i=4),
         in_=planes.rearrange("p t (c i) -> p c t i", i=4),
-    )
-
-
-def regroup_on_gpsimd(nc, grouped, planes):
-    nc.gpsimd.tensor_scalar(
-        out=grouped[:],
-        in0=planes.rearrange("p t c -> p c t"),
-        scalar1=1.0,
-        scalar2=0.0,
-        op0=MULT,
-        op1=ADD,
     )
 
 
@@ -61,7 +51,10 @@ def tile_sage_re_pa_kernel(tc, x, adj, alpha, rezero_w, out):
         psum_wide = pools.enter_context(tc.psum_pool(name="psum_wide", bufs=4))
         psum_work = pools.enter_context(tc.psum_pool(name="psum_work", bufs=4))
 
+        x_view = x.rearrange("(a p) c -> p a c", p=P)
         adj_cols = []
+        x_rows = []
+        w_rows = keep.tile([P, PACK, FEATURES], BF16)
         for s in range(GROUPS):
             adj_view = adj[:, s * GROUP : (s + 1) * GROUP].rearrange("(a p) f -> p a f", p=P)
             pieces = []
@@ -70,14 +63,14 @@ def tile_sage_re_pa_kernel(tc, x, adj, alpha, rezero_w, out):
                 nc.sync.dma_start(out=piece[:], in_=adj_view[:, q * PACK : (q + 1) * PACK, :])
                 pieces.append(piece)
             adj_cols.append(pieces)
-        x_view = x.rearrange("(a p) c -> p a c", p=P)
-        x_rows = []
-        for h in range(GROUPS):
-            x_h = keep.tile([P, PACK, FEATURES], BF16, name="x_rows%d" % h)
-            nc.sync.dma_start(out=x_h[:], in_=x_view[:, h * PACK : (h + 1) * PACK, :])
-            x_rows.append(x_h)
-        w_rows = keep.tile([P, PACK, FEATURES], BF16)
-        nc.sync.dma_start(out=w_rows[:], in_=rezero_w.rearrange("(t p) n -> p t n", p=P))
+            if s == GROUPS_BEFORE_X - 1:
+                for h in range(GROUPS):
+                    x_h = keep.tile([P, PACK, FEATURES], BF16, name="x_rows%d" % h)
+                    nc.sync.dma_start(out=x_h[:], in_=x_view[:, h * PACK : (h + 1) * PACK, :])
+                    x_rows.append(x_h)
+                nc.sync.dma_start(
+                    out=w_rows[:], in_=rezero_w.rearrange("(t p) n -> p t n", p=P)
+                )
         alpha_bf = keep.tile([P, 1], BF16)
         nc.scalar.dma_start(out=alpha_bf[:], in_=alpha.partition_broadcast(P))
 
@@ -131,14 +124,14 @@ def tile_sage_re_pa_kernel(tc, x, adj, alpha, rezero_w, out):
         x_scales = []
         for h in range(GROUPS):
             x_grouped = x_stage.tile([P, FEATURES, PACK], BF16, align_bytes=64)
-            regroup_on_gpsimd(nc, x_grouped, x_rows[h])
+            regroup(nc.scalar.copy, x_grouped, x_rows[h])
             x_codes.append(keep.tile([P, FEATURES], U32, name="x_codes%d" % h, align_bytes=64))
             x_scales.append(keep.tile([P, FEATURES], U8, name="x_scales%d" % h, align_bytes=64))
             quantise(nc, x_grouped, x_codes[h][:], x_scales[h][:])
         w_codes = keep.tile([P, FEATURES], U32, align_bytes=64)
         w_scales = keep.tile([P, FEATURES], U8, align_bytes=64)
         w_grouped = keep.tile([P, FEATURES, PACK], BF16, align_bytes=64)
-        regroup_on_gpsimd(nc, w_grouped, w_rows)
+        regroup(nc.scalar.copy, w_grouped, w_rows)
         quantise(nc, w_grouped, w_codes[:], w_scales[:])
 
         n_codes = {}
@@ -164,7 +157,7 @@ def tile_sage_re_pa_kernel(tc, x, adj, alpha, rezero_w, out):
                     op1=MULT,
                 )
             direct = stage.tile([P, GROUP, PACK], BF16, align_bytes=64)
-            regroup(nc.scalar.copy, direct, square)
+            regroup(nc.vector.tensor_copy if g == s else nc.scalar.copy, direct, square)
             if g == s:
                 return direct, None
             mirrored = stage.tile([P, GROUP, PACK], BF16, align_bytes=64)
@@ -190,7 +183,8 @@ def tile_sage_re_pa_kernel(tc, x, adj, alpha, rezero_w, out):
             if mirrored is not None:
                 quantise(nc, mirrored, n_codes[s, g][:], n_scales[s, g][:])
 
-        agg_grouped = {}
+        agg_codes = {}
+        agg_scales = {}
 
         def aggregate_rows(r, b):
             cols = slice(b * P, (b + 1) * P)
@@ -206,22 +200,24 @@ def tile_sage_re_pa_kernel(tc, x, adj, alpha, rezero_w, out):
                         start=(h == 0),
                         stop=(h == GROUPS - 1),
                     )
-            agg_grouped[r, b] = agg_pool.tile(
-                [P, P, PACK], BF16, name="agg_grouped_%d_%d" % (r, b), align_bytes=64
+            agg_grouped = rows_pool.tile([P, P, PACK], BF16, align_bytes=64)
+            nc.scalar.copy(out=agg_grouped[:], in_=agg_t.rearrange("p t m -> p m t"))
+            agg_codes[r, b] = agg_pool.tile(
+                [P, P], U32, name="agg_codes_%d_%d" % (r, b), align_bytes=64
             )
-            nc.scalar.copy(out=agg_grouped[r, b][:], in_=agg_t.rearrange("p t m -> p m t"))
+            agg_scales[r, b] = agg_pool.tile(
+                [P, P], U8, name="agg_scales_%d_%d" % (r, b), align_bytes=64
+            )
+            quantise(nc, agg_grouped, agg_codes[r, b][:], agg_scales[r, b][:])
 
         products = {}
 
         def second_matmul(r, b):
-            agg_codes = rows_pool.tile([P, P], U32, align_bytes=64)
-            agg_scales = rows_pool.tile([P, P], U8, align_bytes=64)
-            quantise(nc, agg_grouped[r, b], agg_codes[:], agg_scales[:])
             product = psum_wide.tile([P, FEATURES], F32, tag="wide")
             nc.tensor.matmul_mx(
                 out=product[:],
-                lhsT=agg_codes[:].bitcast(FP8X4),
-                lhsT_scale=agg_scales[:],
+                lhsT=agg_codes[r, b][:].bitcast(FP8X4),
+                lhsT_scale=agg_scales[r, b][:],
                 rhs=w_codes[:].bitcast(FP8X4),
                 rhs_scale=w_scales[:],
                 start=True,

@@ -44,7 +44,7 @@ def tile_sage_re_pa_kernel(tc, x, adj, alpha, rezero_w, out):
     nc = tc.nc
     with ExitStack() as pools:
         keep = pools.enter_context(tc.tile_pool(name="keep", bufs=1))
-        stage = pools.enter_context(tc.tile_pool(name="stage", bufs=3))
+        stage = pools.enter_context(tc.tile_pool(name="stage", bufs=4))
         x_stage = pools.enter_context(tc.tile_pool(name="x_stage", bufs=2))
         rows_pool = pools.enter_context(tc.tile_pool(name="rows_pool", bufs=6))
         agg_pool = pools.enter_context(tc.tile_pool(name="agg_pool", bufs=1))
@@ -147,6 +147,9 @@ def tile_sage_re_pa_kernel(tc, x, adj, alpha, rezero_w, out):
 
         def normalise_square(g, s):
             square = stage.tile([P, PACK, GROUP], BF16)
+            mirrored = None
+            if g < s:
+                mirrored = stage.tile([P, GROUP, PACK], BF16, align_bytes=64)
             for t in range(PACK):
                 nc.vector.scalar_tensor_tensor(
                     out=square[:, t, :],
@@ -156,32 +159,21 @@ def tile_sage_re_pa_kernel(tc, x, adj, alpha, rezero_w, out):
                     op0=MULT,
                     op1=MULT,
                 )
-            direct = stage.tile([P, GROUP, PACK], BF16, align_bytes=64)
-            regroup(nc.vector.tensor_copy if g == s else nc.scalar.copy, direct, square)
-            if g == s:
-                return direct, None
-            mirrored = stage.tile([P, GROUP, PACK], BF16, align_bytes=64)
-            for half in range(2):
-                flipped = psum_work.tile([P, 2, PACK, P], BF16, tag="work")
-                for u in range(2):
+                if g < s:
+                    flipped = psum_work.tile([P, PACK, P], BF16, tag="work")
                     for tj in range(PACK):
                         nc.tensor.transpose(
-                            out=flipped[:, u, tj, :],
-                            in_=square[:, 2 * half + u, tj * P : (tj + 1) * P],
+                            out=flipped[:, tj, :],
+                            in_=square[:, t, tj * P : (tj + 1) * P],
                             identity=ident_bf[:],
                         )
-                nc.scalar.copy(
-                    out=mirrored[:, 2 * half * P : 2 * (half + 1) * P, :].rearrange(
-                        "p (u m) t -> p u m t", u=2
-                    ),
-                    in_=flipped.rearrange("p u t m -> p u m t"),
-                )
+                    nc.scalar.copy(
+                        out=mirrored[:, t * P : (t + 1) * P, :],
+                        in_=flipped.rearrange("p tj m -> p m tj"),
+                    )
+            direct = stage.tile([P, GROUP, PACK], BF16, align_bytes=64)
+            regroup(nc.vector.tensor_copy if g == s else nc.scalar.copy, direct, square)
             return direct, mirrored
-
-        def quantise_square(g, s, direct, mirrored):
-            quantise(nc, direct, n_codes[g, s][:], n_scales[g, s][:])
-            if mirrored is not None:
-                quantise(nc, mirrored, n_codes[s, g][:], n_scales[s, g][:])
 
         agg_codes = {}
         agg_scales = {}
@@ -209,6 +201,15 @@ def tile_sage_re_pa_kernel(tc, x, adj, alpha, rezero_w, out):
                 [P, P], U8, name="agg_scales_%d_%d" % (r, b), align_bytes=64
             )
             quantise(nc, agg_grouped, agg_codes[r, b][:], agg_scales[r, b][:])
+
+        def quantise_square(g, s, direct, mirrored):
+            quantise(nc, direct, n_codes[g, s][:], n_scales[g, s][:])
+            for b in range(PACK):
+                cols = slice(b * P, (b + 1) * P)
+                if g < s:
+                    quantise(nc, mirrored[:, cols, :], n_codes[s, g][:, cols], n_scales[s, g][:, cols])
+                if s == GROUPS - 1:
+                    aggregate_rows(g, b)
 
         products = {}
 
@@ -250,9 +251,6 @@ def tile_sage_re_pa_kernel(tc, x, adj, alpha, rezero_w, out):
             if n > 0:
                 g, s = squares[n - 1]
                 quantise_square(g, s, *grouped[n - 1])
-                if s == GROUPS - 1:
-                    for b in range(PACK):
-                        aggregate_rows(g, b)
 
         blocks = [(r, b) for r in range(GROUPS) for b in range(PACK)]
         with tc.manual_schedule():

@@ -51,22 +51,28 @@ def tile_sage_re_pa_kernel(tc, x, adj, alpha, rezero_w, out):
         psum_wide = pools.enter_context(tc.psum_pool(name="psum_wide", bufs=4))
         psum_work = pools.enter_context(tc.psum_pool(name="psum_work", bufs=4))
 
-        x_view = x.rearrange("(a p) c -> p a c", p=P)
+        x_view = x.rearrange("(h u p e) c -> h p u e c", u=2, p=P, e=2)
+        out_view = out.rearrange("(r u p e) c -> r u e p c", u=2, p=P, e=2)
         adj_cols = []
         x_rows = []
         w_rows = keep.tile([P, PACK, FEATURES], BF16)
         for s in range(GROUPS):
-            adj_view = adj[:, s * GROUP : (s + 1) * GROUP].rearrange("(a p) f -> p a f", p=P)
+            adj_view = adj[:, s * GROUP : (s + 1) * GROUP].rearrange(
+                "(q u p e) f -> q u p e f", u=2, p=P, e=2
+            )
             pieces = []
             for q in range(GROUPS):
                 piece = keep.tile([P, PACK, GROUP], BF16, name="adj_%d_%d" % (q, s))
-                nc.sync.dma_start(out=piece[:], in_=adj_view[:, q * PACK : (q + 1) * PACK, :])
+                for u in range(2):
+                    nc.sync.dma_start(out=piece[:, 2 * u : 2 * u + 2, :], in_=adj_view[q, u])
                 pieces.append(piece)
             adj_cols.append(pieces)
             if s == GROUPS_BEFORE_X - 1:
                 for h in range(GROUPS):
                     x_h = keep.tile([P, PACK, FEATURES], BF16, name="x_rows%d" % h)
-                    nc.sync.dma_start(out=x_h[:], in_=x_view[:, h * PACK : (h + 1) * PACK, :])
+                    nc.sync.dma_start(
+                        out=x_h.rearrange("p (u e) c -> p u e c", e=2), in_=x_view[h]
+                    )
                     x_rows.append(x_h)
                 nc.sync.dma_start(
                     out=w_rows[:], in_=rezero_w.rearrange("(t p) n -> p t n", p=P)
@@ -76,8 +82,6 @@ def tile_sage_re_pa_kernel(tc, x, adj, alpha, rezero_w, out):
 
         ones = keep.tile([P, ONES_WIDTH], BF16)
         nc.vector.memset(ones[:], 1.0)
-        ident_bf = keep.tile([P, P], BF16)
-        make_identity(nc, ident_bf[:])
         ident_f32 = keep.tile([P, P], F32)
         make_identity(nc, ident_f32[:])
         alpha_f32 = keep.tile([P, 1], F32)
@@ -90,11 +94,12 @@ def tile_sage_re_pa_kernel(tc, x, adj, alpha, rezero_w, out):
         for s in range(GROUPS):
             part = psum_work.tile([P, GROUPS, PACK, ONES_WIDTH], F32, tag="work")
             for q in range(GROUPS):
+                columns = adj_cols[s][q].rearrange("p t (u m e) -> p t u e m", u=2, e=2)
                 for b in range(PACK):
                     for t in range(PACK):
                         nc.tensor.matmul(
                             out=part[:, q, b, :],
-                            lhsT=adj_cols[s][q][:, t, b * P : (b + 1) * P],
+                            lhsT=columns[:, t, b // 2, b % 2, :],
                             rhs=ones[:],
                             start=(t == 0),
                             stop=(t == PACK - 1),
@@ -112,9 +117,10 @@ def tile_sage_re_pa_kernel(tc, x, adj, alpha, rezero_w, out):
             nc.scalar.activation(out=col_s[:], in_=inverse[:], func=SQRT)
             dis_col.append(col_s)
             row_s = psum_wide.tile([P, GROUP], F32, tag="wide")
+            row_view = row_s.rearrange("p (u m e) -> p u e m", u=2, e=2)
             for b in range(PACK):
                 nc.tensor.transpose(
-                    out=row_s[:, b * P : (b + 1) * P],
+                    out=row_view[:, b // 2, b % 2, :],
                     in_=col_s[:, b : b + 1].to_broadcast([P, P]),
                     identity=ident_f32[:],
                 )
@@ -147,32 +153,44 @@ def tile_sage_re_pa_kernel(tc, x, adj, alpha, rezero_w, out):
 
         def normalise_square(g, s):
             square = stage.tile([P, PACK, GROUP], BF16)
-            mirrored = None
-            if g < s:
-                mirrored = stage.tile([P, GROUP, PACK], BF16, align_bytes=64)
-            for t in range(PACK):
-                nc.vector.scalar_tensor_tensor(
-                    out=square[:, t, :],
-                    in0=adj_cols[s][g][:, t, :],
-                    scalar=dis_col[g][:, t : t + 1],
-                    in1=dis_row[s][:],
-                    op0=MULT,
-                    op1=MULT,
-                )
-                if g < s:
-                    flipped = psum_work.tile([P, PACK, P], BF16, tag="work")
-                    for tj in range(PACK):
-                        nc.tensor.transpose(
-                            out=flipped[:, tj, :],
-                            in_=square[:, t, tj * P : (tj + 1) * P],
-                            identity=ident_bf[:],
-                        )
-                    nc.scalar.copy(
-                        out=mirrored[:, t * P : (t + 1) * P, :],
-                        in_=flipped.rearrange("p tj m -> p m tj"),
+            mirrored = stage.tile([P, GROUP, PACK], BF16, align_bytes=64)
+            mirrored_words = (
+                mirrored.rearrange("p c t -> p (c t)")
+                .bitcast(F32)
+                .rearrange("p (c u) -> p c u", u=2)
+            )
+            for half in range(2):
+                flipped = psum_work.tile([P, 2, 2, P], F32, tag="work")
+                for e in range(2):
+                    t = 2 * half + e
+                    nc.vector.scalar_tensor_tensor(
+                        out=square[:, t, :],
+                        in0=adj_cols[s][g][:, t, :],
+                        scalar=dis_col[g][:, t : t + 1],
+                        in1=dis_row[s][:],
+                        op0=MULT,
+                        op1=MULT,
                     )
+                    words = square[:, t, :].bitcast(F32)
+                    for u in range(2):
+                        nc.tensor.transpose(
+                            out=flipped[:, e, u, :],
+                            in_=words[:, u * P : (u + 1) * P],
+                            identity=ident_f32[:],
+                        )
+                for e in range(2):
+                    t = 2 * half + e
+                    nc.scalar.copy(
+                        out=mirrored_words[:, t * P : (t + 1) * P, :],
+                        in_=flipped[:, e].rearrange("p u m -> p m u"),
+                    )
+            if g == s:
+                return None, mirrored
             direct = stage.tile([P, GROUP, PACK], BF16, align_bytes=64)
-            regroup(nc.vector.tensor_copy if g == s else nc.scalar.copy, direct, square)
+            direct_view = direct.rearrange("p (u e m) t -> p u m t e", u=2, e=2)
+            square_view = square.rearrange("p t (u m e) -> p u m t e", u=2, e=2)
+            for u in range(2):
+                nc.scalar.copy(out=direct_view[:, u], in_=square_view[:, u])
             return direct, mirrored
 
         agg_codes = {}
@@ -203,13 +221,14 @@ def tile_sage_re_pa_kernel(tc, x, adj, alpha, rezero_w, out):
             quantise(nc, agg_grouped, agg_codes[r, b][:], agg_scales[r, b][:])
 
         def quantise_square(g, s, direct, mirrored):
-            quantise(nc, direct, n_codes[g, s][:], n_scales[g, s][:])
-            for b in range(PACK):
-                cols = slice(b * P, (b + 1) * P)
-                if g < s:
-                    quantise(nc, mirrored[:, cols, :], n_codes[s, g][:, cols], n_scales[s, g][:, cols])
+            if g < s:
+                quantise(nc, direct, n_codes[g, s][:], n_scales[g, s][:])
+            for half in range(2):
+                cols = slice(half * 2 * P, (half + 1) * 2 * P)
+                quantise(nc, mirrored[:, cols, :], n_codes[s, g][:, cols], n_scales[s, g][:, cols])
                 if s == GROUPS - 1:
-                    aggregate_rows(g, b)
+                    aggregate_rows(g, 2 * half)
+                    aggregate_rows(g, 2 * half + 1)
 
         products = {}
 
@@ -227,7 +246,6 @@ def tile_sage_re_pa_kernel(tc, x, adj, alpha, rezero_w, out):
             products[r, b] = product
 
         def add_residual(r, b):
-            first = r * GROUP + b * P
             result = rows_pool.tile([P, FEATURES], F32)
             nc.vector.scalar_tensor_tensor(
                 out=result[:],
@@ -237,7 +255,7 @@ def tile_sage_re_pa_kernel(tc, x, adj, alpha, rezero_w, out):
                 op0=MULT,
                 op1=ADD,
             )
-            nc.sync.dma_start(out=out[first : first + P, :], in_=result[:])
+            nc.sync.dma_start(out=out_view[r, b // 2, b % 2], in_=result[:])
 
         squares = [
             (g, diagonal - g)

@@ -20,7 +20,7 @@ FEATURES = 512
 GROUPS = NODES // GROUP
 ONES_WIDTH = 32
 GROUPS_BEFORE_X = 2
-AHEAD = 3
+LAG = 1
 
 FLOPS = 2 * NODES * NODES * FEATURES + 2 * NODES * FEATURES * FEATURES
 
@@ -51,28 +51,23 @@ def tile_sage_re_pa_kernel(tc, x, adj, alpha, rezero_w, out):
         psum_wide = pools.enter_context(tc.psum_pool(name="psum_wide", bufs=4))
         psum_work = pools.enter_context(tc.psum_pool(name="psum_work", bufs=4))
 
-        x_view = x.rearrange("(h u p e) c -> h p u e c", u=2, p=P, e=2)
-        out_view = out.rearrange("(r u p e) c -> r u e p c", u=2, p=P, e=2)
+        x_view = x.rearrange("(h e v p) c -> h v p e c", e=2, v=2, p=P)
         adj_cols = []
         x_rows = []
         w_rows = keep.tile([P, PACK, FEATURES], BF16)
         for s in range(GROUPS):
-            adj_view = adj[:, s * GROUP : (s + 1) * GROUP].rearrange(
-                "(q u p e) f -> q u p e f", u=2, p=P, e=2
-            )
+            adj_view = adj[:, s * GROUP : (s + 1) * GROUP].rearrange("(a p) f -> p a f", p=P)
             pieces = []
             for q in range(GROUPS):
                 piece = keep.tile([P, PACK, GROUP], BF16, name="adj_%d_%d" % (q, s))
-                for u in range(2):
-                    nc.sync.dma_start(out=piece[:, 2 * u : 2 * u + 2, :], in_=adj_view[q, u])
+                nc.sync.dma_start(out=piece[:], in_=adj_view[:, q * PACK : (q + 1) * PACK, :])
                 pieces.append(piece)
             adj_cols.append(pieces)
             if s == GROUPS_BEFORE_X - 1:
                 for h in range(GROUPS):
-                    x_h = keep.tile([P, PACK, FEATURES], BF16, name="x_rows%d" % h)
-                    nc.sync.dma_start(
-                        out=x_h.rearrange("p (u e) c -> p u e c", e=2), in_=x_view[h]
-                    )
+                    x_h = keep.tile([P, 2, 2, FEATURES], BF16, name="x_rows%d" % h)
+                    for v in range(2):
+                        nc.sync.dma_start(out=x_h[:, v], in_=x_view[h, v])
                     x_rows.append(x_h)
                 nc.sync.dma_start(
                     out=w_rows[:], in_=rezero_w.rearrange("(t p) n -> p t n", p=P)
@@ -94,12 +89,11 @@ def tile_sage_re_pa_kernel(tc, x, adj, alpha, rezero_w, out):
         for s in range(GROUPS):
             part = psum_work.tile([P, GROUPS, PACK, ONES_WIDTH], F32, tag="work")
             for q in range(GROUPS):
-                columns = adj_cols[s][q].rearrange("p t (u m e) -> p t u e m", u=2, e=2)
                 for b in range(PACK):
                     for t in range(PACK):
                         nc.tensor.matmul(
                             out=part[:, q, b, :],
-                            lhsT=columns[:, t, b // 2, b % 2, :],
+                            lhsT=adj_cols[s][q][:, t, b * P : (b + 1) * P],
                             rhs=ones[:],
                             start=(t == 0),
                             stop=(t == PACK - 1),
@@ -116,11 +110,10 @@ def tile_sage_re_pa_kernel(tc, x, adj, alpha, rezero_w, out):
             col_s = keep.tile([P, PACK], F32, name="dis_col%d" % s)
             nc.scalar.activation(out=col_s[:], in_=inverse[:], func=SQRT)
             dis_col.append(col_s)
-            row_s = psum_wide.tile([P, GROUP], F32, tag="wide")
-            row_view = row_s.rearrange("p (u m e) -> p u e m", u=2, e=2)
+            row_s = psum_wide.tile([P, 2 * P, 2], F32, tag="wide")
             for b in range(PACK):
                 nc.tensor.transpose(
-                    out=row_view[:, b // 2, b % 2, :],
+                    out=row_s[:, b % 2 * P : (b % 2 + 1) * P, b // 2],
                     in_=col_s[:, b : b + 1].to_broadcast([P, P]),
                     identity=ident_f32[:],
                 )
@@ -130,7 +123,7 @@ def tile_sage_re_pa_kernel(tc, x, adj, alpha, rezero_w, out):
         x_scales = []
         for h in range(GROUPS):
             x_grouped = x_stage.tile([P, FEATURES, PACK], BF16, align_bytes=64)
-            regroup(nc.scalar.copy, x_grouped, x_rows[h])
+            regroup(nc.scalar.copy, x_grouped, x_rows[h].rearrange("p v e c -> p (v e) c"))
             x_codes.append(keep.tile([P, FEATURES], U32, name="x_codes%d" % h, align_bytes=64))
             x_scales.append(keep.tile([P, FEATURES], U8, name="x_scales%d" % h, align_bytes=64))
             quantise(nc, x_grouped, x_codes[h][:], x_scales[h][:])
@@ -152,45 +145,41 @@ def tile_sage_re_pa_kernel(tc, x, adj, alpha, rezero_w, out):
                 )
 
         def normalise_square(g, s):
-            square = stage.tile([P, PACK, GROUP], BF16)
+            square = stage.tile([P, PACK, 2 * P, 2], BF16)
             mirrored = stage.tile([P, GROUP, PACK], BF16, align_bytes=64)
             mirrored_words = (
                 mirrored.rearrange("p c t -> p (c t)")
                 .bitcast(F32)
-                .rearrange("p (c u) -> p c u", u=2)
+                .rearrange("p (c v) -> p c v", v=2)
             )
-            for half in range(2):
-                flipped = psum_work.tile([P, 2, 2, P], F32, tag="work")
-                for e in range(2):
-                    t = 2 * half + e
-                    nc.vector.scalar_tensor_tensor(
-                        out=square[:, t, :],
-                        in0=adj_cols[s][g][:, t, :],
-                        scalar=dis_col[g][:, t : t + 1],
-                        in1=dis_row[s][:],
-                        op0=MULT,
-                        op1=MULT,
+            for t in range(PACK):
+                nc.vector.scalar_tensor_tensor(
+                    out=square[:, t],
+                    in0=adj_cols[s][g][:, t, :].rearrange("p (e w) -> p w e", e=2),
+                    scalar=dis_col[g][:, t : t + 1],
+                    in1=dis_row[s][:],
+                    op0=MULT,
+                    op1=MULT,
+                )
+                words = square[:, t].rearrange("p w e -> p (w e)").bitcast(F32)
+                flipped = psum_work.tile([P, 2, P], F32, tag="work")
+                for v in range(2):
+                    nc.tensor.transpose(
+                        out=flipped[:, v, :],
+                        in_=words[:, v * P : (v + 1) * P],
+                        identity=ident_f32[:],
                     )
-                    words = square[:, t, :].bitcast(F32)
-                    for u in range(2):
-                        nc.tensor.transpose(
-                            out=flipped[:, e, u, :],
-                            in_=words[:, u * P : (u + 1) * P],
-                            identity=ident_f32[:],
-                        )
-                for e in range(2):
-                    t = 2 * half + e
-                    nc.scalar.copy(
-                        out=mirrored_words[:, t * P : (t + 1) * P, :],
-                        in_=flipped[:, e].rearrange("p u m -> p m u"),
-                    )
+                nc.scalar.copy(
+                    out=mirrored_words[:, t * P : (t + 1) * P, :],
+                    in_=flipped.rearrange("p v i -> p i v"),
+                )
             if g == s:
                 return None, mirrored
             direct = stage.tile([P, GROUP, PACK], BF16, align_bytes=64)
-            direct_view = direct.rearrange("p (u e m) t -> p u m t e", u=2, e=2)
-            square_view = square.rearrange("p t (u m e) -> p u m t e", u=2, e=2)
-            for u in range(2):
-                nc.scalar.copy(out=direct_view[:, u], in_=square_view[:, u])
+            direct_view = direct.rearrange("p (half w) (v e) -> p half w v e", half=2, e=2)
+            square_view = square.rearrange("p (e v) w half -> p half w v e", e=2)
+            for half in range(2):
+                nc.scalar.copy(out=direct_view[:, half], in_=square_view[:, half])
             return direct, mirrored
 
         agg_codes = {}
@@ -223,12 +212,13 @@ def tile_sage_re_pa_kernel(tc, x, adj, alpha, rezero_w, out):
         def quantise_square(g, s, direct, mirrored):
             if g < s:
                 quantise(nc, direct, n_codes[g, s][:], n_scales[g, s][:])
-            for half in range(2):
-                cols = slice(half * 2 * P, (half + 1) * 2 * P)
+            if s < GROUPS - 1:
+                quantise(nc, mirrored, n_codes[s, g][:], n_scales[s, g][:])
+                return
+            for b in range(PACK):
+                cols = slice(b * P, (b + 1) * P)
                 quantise(nc, mirrored[:, cols, :], n_codes[s, g][:, cols], n_scales[s, g][:, cols])
-                if s == GROUPS - 1:
-                    aggregate_rows(g, 2 * half)
-                    aggregate_rows(g, 2 * half + 1)
+                aggregate_rows(g, b)
 
         products = {}
 
@@ -246,16 +236,17 @@ def tile_sage_re_pa_kernel(tc, x, adj, alpha, rezero_w, out):
             products[r, b] = product
 
         def add_residual(r, b):
+            first = r * GROUP + b * P
             result = rows_pool.tile([P, FEATURES], F32)
             nc.vector.scalar_tensor_tensor(
                 out=result[:],
                 in0=products[r, b][:],
                 scalar=alpha_f32[:, 0:1],
-                in1=x_rows[r][:, b, :],
+                in1=x_rows[r][:, b % 2, b // 2, :],
                 op0=MULT,
                 op1=ADD,
             )
-            nc.sync.dma_start(out=out_view[r, b // 2, b % 2], in_=result[:])
+            nc.sync.dma_start(out=out[first : first + P, :], in_=result[:])
 
         squares = [
             (g, diagonal - g)
@@ -263,17 +254,14 @@ def tile_sage_re_pa_kernel(tc, x, adj, alpha, rezero_w, out):
             for g in range(max(0, diagonal - GROUPS + 1), diagonal // 2 + 1)
         ]
         grouped = {}
-        for n in range(len(squares) + 1):
+        for n in range(len(squares) + 1 + LAG):
             if n < len(squares):
                 grouped[n] = normalise_square(*squares[n])
-            if n > 0:
-                g, s = squares[n - 1]
-                quantise_square(g, s, *grouped[n - 1])
-
-        blocks = [(r, b) for r in range(GROUPS) for b in range(PACK)]
-        with tc.manual_schedule():
-            for k in range(len(blocks) + AHEAD):
-                if k < len(blocks):
-                    second_matmul(*blocks[k])
-                if k >= AHEAD:
-                    add_residual(*blocks[k - AHEAD])
+            if 0 < n <= len(squares):
+                quantise_square(*squares[n - 1], *grouped[n - 1])
+            if n > LAG:
+                r, last = squares[n - 1 - LAG]
+                if last == GROUPS - 1:
+                    for b in range(PACK):
+                        second_matmul(r, b)
+                        add_residual(r, b)

@@ -19,8 +19,8 @@ NODES = 2048
 FEATURES = 512
 GROUPS = NODES // GROUP
 ONES_WIDTH = 32
-GROUPS_BEFORE_X = 2
-LAG = 1
+X_AFTER = {1: (0, 1), 2: (2, 3)}
+W_AFTER = 2
 
 FLOPS = 2 * NODES * NODES * FEATURES + 2 * NODES * FEATURES * FEATURES
 
@@ -30,6 +30,10 @@ def regroup(engine_copy, grouped, planes):
         out=grouped.rearrange("p (c i) t -> p c t i", i=4),
         in_=planes.rearrange("p t (c i) -> p c t i", i=4),
     )
+
+
+def place(t):
+    return 2 * (t % 2) + t // 2
 
 
 def quantise(nc, grouped, codes, scales):
@@ -44,11 +48,13 @@ def tile_sage_re_pa_kernel(tc, x, adj, alpha, rezero_w, out):
     nc = tc.nc
     with ExitStack() as pools:
         keep = pools.enter_context(tc.tile_pool(name="keep", bufs=1))
-        stage = pools.enter_context(tc.tile_pool(name="stage", bufs=4))
+        stage = pools.enter_context(tc.tile_pool(name="stage", bufs=3))
         x_stage = pools.enter_context(tc.tile_pool(name="x_stage", bufs=2))
+        square_pool = pools.enter_context(tc.tile_pool(name="square_pool", bufs=8))
         rows_pool = pools.enter_context(tc.tile_pool(name="rows_pool", bufs=6))
         agg_pool = pools.enter_context(tc.tile_pool(name="agg_pool", bufs=1))
-        psum_wide = pools.enter_context(tc.psum_pool(name="psum_wide", bufs=4))
+        psum_sums = pools.enter_context(tc.psum_pool(name="psum_sums", bufs=1))
+        psum_wide = pools.enter_context(tc.psum_pool(name="psum_wide", bufs=3))
         psum_work = pools.enter_context(tc.psum_pool(name="psum_work", bufs=4))
 
         x_view = x.rearrange("(h e v p) c -> h v p e c", e=2, v=2, p=P)
@@ -63,12 +69,13 @@ def tile_sage_re_pa_kernel(tc, x, adj, alpha, rezero_w, out):
                 nc.sync.dma_start(out=piece[:], in_=adj_view[:, q * PACK : (q + 1) * PACK, :])
                 pieces.append(piece)
             adj_cols.append(pieces)
-            if s == GROUPS_BEFORE_X - 1:
-                for h in range(GROUPS):
-                    x_h = keep.tile([P, 2, 2, FEATURES], BF16, name="x_rows%d" % h)
+            if s in X_AFTER:
+                for h in X_AFTER[s]:
+                    x_h = keep.tile([P, PACK, FEATURES], BF16, name="x_rows%d" % h)
                     for v in range(2):
-                        nc.sync.dma_start(out=x_h[:, v], in_=x_view[h, v])
+                        nc.sync.dma_start(out=x_h[:, 2 * v : 2 * v + 2, :], in_=x_view[h, v])
                     x_rows.append(x_h)
+            if s == W_AFTER:
                 nc.sync.dma_start(
                     out=w_rows[:], in_=rezero_w.rearrange("(t p) n -> p t n", p=P)
                 )
@@ -80,28 +87,31 @@ def tile_sage_re_pa_kernel(tc, x, adj, alpha, rezero_w, out):
         ident_f32 = keep.tile([P, P], F32)
         make_identity(nc, ident_f32[:])
         alpha_f32 = keep.tile([P, 1], F32)
-        nc.vector.tensor_copy(out=alpha_f32[:], in_=alpha_bf[:])
         warm = keep.tile([P, 1], F32)
         nc.scalar.activation(out=warm[:], in_=ones[:, 0:1], func=SQRT)
 
         dis_col = []
         dis_row = []
-        for s in range(GROUPS):
-            part = psum_work.tile([P, GROUPS, PACK, ONES_WIDTH], F32, tag="work")
-            for q in range(GROUPS):
-                for b in range(PACK):
-                    for t in range(PACK):
-                        nc.tensor.matmul(
-                            out=part[:, q, b, :],
-                            lhsT=adj_cols[s][q][:, t, b * P : (b + 1) * P],
-                            rhs=ones[:],
-                            start=(t == 0),
-                            stop=(t == PACK - 1),
-                        )
+        parts = {}
+
+        def degree_sums(s, q):
+            if q == 0:
+                parts[s] = psum_sums.tile([P, GROUPS, PACK, ONES_WIDTH], F32, tag="sums", name="part")
+            for b in range(PACK):
+                for t in range(PACK):
+                    nc.tensor.matmul(
+                        out=parts[s][:, q, b, :],
+                        lhsT=adj_cols[s][q][:, t, b * P : (b + 1) * P],
+                        rhs=ones[:],
+                        start=(t == 0),
+                        stop=(t == PACK - 1),
+                    )
+
+        def degrees(s):
             deg = stage.tile([P, PACK], F32)
             nc.vector.tensor_reduce(
                 out=deg[:],
-                in_=part[:, :, :, 0].rearrange("p q b -> p b q"),
+                in_=parts[s][:, :, :, 0].rearrange("p q b -> p b q"),
                 axis=mybir.AxisListType.X,
                 op=ADD,
             )
@@ -122,16 +132,24 @@ def tile_sage_re_pa_kernel(tc, x, adj, alpha, rezero_w, out):
         x_codes = []
         x_scales = []
         for h in range(GROUPS):
-            x_grouped = x_stage.tile([P, FEATURES, PACK], BF16, align_bytes=64)
-            regroup(nc.scalar.copy, x_grouped, x_rows[h].rearrange("p v e c -> p (v e) c"))
             x_codes.append(keep.tile([P, FEATURES], U32, name="x_codes%d" % h, align_bytes=64))
             x_scales.append(keep.tile([P, FEATURES], U8, name="x_scales%d" % h, align_bytes=64))
-            quantise(nc, x_grouped, x_codes[h][:], x_scales[h][:])
         w_codes = keep.tile([P, FEATURES], U32, align_bytes=64)
         w_scales = keep.tile([P, FEATURES], U8, align_bytes=64)
-        w_grouped = keep.tile([P, FEATURES, PACK], BF16, align_bytes=64)
-        regroup(nc.scalar.copy, w_grouped, w_rows)
-        quantise(nc, w_grouped, w_codes[:], w_scales[:])
+        x_grouped = {}
+
+        def regroup_half(h, half):
+            if half == 0:
+                x_grouped[h] = x_stage.tile([P, FEATURES, PACK], BF16, align_bytes=64, name="x_grouped")
+            cols = slice(half * FEATURES // 2, (half + 1) * FEATURES // 2)
+            planes = x_rows[h] if h < GROUPS else w_rows
+            regroup(nc.scalar.copy, x_grouped[h][:, cols, :], planes[:, :, cols])
+
+        def quantise_x(h):
+            quantise(nc, x_grouped[h], x_codes[h][:], x_scales[h][:])
+
+        def quantise_w():
+            quantise(nc, x_grouped[GROUPS], w_codes[:], w_scales[:])
 
         n_codes = {}
         n_scales = {}
@@ -144,8 +162,12 @@ def tile_sage_re_pa_kernel(tc, x, adj, alpha, rezero_w, out):
                     [P, GROUP], U8, name="n_scales_%d_%d" % (h, r), align_bytes=64
                 )
 
-        def normalise_square(g, s):
-            square = stage.tile([P, PACK, 2 * P, 2], BF16)
+        squares = {}
+        mirrors = {}
+        directs = {}
+
+        def normalise(g, s):
+            square = square_pool.tile([P, PACK, 2 * P, 2], BF16)
             mirrored = stage.tile([P, GROUP, PACK], BF16, align_bytes=64)
             mirrored_words = (
                 mirrored.rearrange("p c t -> p (c t)")
@@ -154,14 +176,14 @@ def tile_sage_re_pa_kernel(tc, x, adj, alpha, rezero_w, out):
             )
             for t in range(PACK):
                 nc.vector.scalar_tensor_tensor(
-                    out=square[:, t],
+                    out=square[:, place(t)],
                     in0=adj_cols[s][g][:, t, :].rearrange("p (e w) -> p w e", e=2),
                     scalar=dis_col[g][:, t : t + 1],
                     in1=dis_row[s][:],
                     op0=MULT,
                     op1=MULT,
                 )
-                words = square[:, t].rearrange("p w e -> p (w e)").bitcast(F32)
+                words = square[:, place(t)].rearrange("p w e -> p (w e)").bitcast(F32)
                 flipped = psum_work.tile([P, 2, P], F32, tag="work")
                 for v in range(2):
                     nc.tensor.transpose(
@@ -173,19 +195,29 @@ def tile_sage_re_pa_kernel(tc, x, adj, alpha, rezero_w, out):
                     out=mirrored_words[:, t * P : (t + 1) * P, :],
                     in_=flipped.rearrange("p v i -> p i v"),
                 )
-            if g == s:
-                return None, mirrored
+            squares[g, s] = square
+            mirrors[g, s] = mirrored
+
+        def regroup_direct(g, s, engine_copy=nc.scalar.copy):
+            square = squares[g, s]
             direct = stage.tile([P, GROUP, PACK], BF16, align_bytes=64)
-            direct_view = direct.rearrange("p (half w) (v e) -> p half w v e", half=2, e=2)
-            square_view = square.rearrange("p (e v) w half -> p half w v e", e=2)
             for half in range(2):
-                nc.scalar.copy(out=direct_view[:, half], in_=square_view[:, half])
-            return direct, mirrored
+                cols = slice(half * 2 * P, (half + 1) * 2 * P)
+                regroup(engine_copy, direct[:, cols, :], square[:, :, :, half])
+            directs[g, s] = direct
+
+        def quantise_direct(g, s):
+            quantise(nc, directs[g, s], n_codes[g, s][:], n_scales[g, s][:])
+
+        def quantise_mirror(g, s, first, count):
+            cols = slice(first * P, (first + count) * P)
+            quantise(nc, mirrors[g, s][:, cols, :], n_codes[s, g][:, cols], n_scales[s, g][:, cols])
 
         agg_codes = {}
         agg_scales = {}
+        agg_grouped = {}
 
-        def aggregate_rows(r, b):
+        def aggregate(r, b):
             cols = slice(b * P, (b + 1) * P)
             agg_t = psum_work.tile([P, PACK, P], F32, tag="work")
             for t in range(PACK):
@@ -199,26 +231,18 @@ def tile_sage_re_pa_kernel(tc, x, adj, alpha, rezero_w, out):
                         start=(h == 0),
                         stop=(h == GROUPS - 1),
                     )
-            agg_grouped = rows_pool.tile([P, P, PACK], BF16, align_bytes=64)
-            nc.scalar.copy(out=agg_grouped[:], in_=agg_t.rearrange("p t m -> p m t"))
+            grouped = rows_pool.tile([P, P, PACK], BF16, align_bytes=64)
+            nc.scalar.copy(out=grouped[:], in_=agg_t.rearrange("p t m -> p m t"))
+            agg_grouped[r, b] = grouped
+
+        def quantise_agg(r, b):
             agg_codes[r, b] = agg_pool.tile(
                 [P, P], U32, name="agg_codes_%d_%d" % (r, b), align_bytes=64
             )
             agg_scales[r, b] = agg_pool.tile(
                 [P, P], U8, name="agg_scales_%d_%d" % (r, b), align_bytes=64
             )
-            quantise(nc, agg_grouped, agg_codes[r, b][:], agg_scales[r, b][:])
-
-        def quantise_square(g, s, direct, mirrored):
-            if g < s:
-                quantise(nc, direct, n_codes[g, s][:], n_scales[g, s][:])
-            if s < GROUPS - 1:
-                quantise(nc, mirrored, n_codes[s, g][:], n_scales[s, g][:])
-                return
-            for b in range(PACK):
-                cols = slice(b * P, (b + 1) * P)
-                quantise(nc, mirrored[:, cols, :], n_codes[s, g][:, cols], n_scales[s, g][:, cols])
-                aggregate_rows(g, b)
+            quantise(nc, agg_grouped[r, b], agg_codes[r, b][:], agg_scales[r, b][:])
 
         products = {}
 
@@ -242,26 +266,126 @@ def tile_sage_re_pa_kernel(tc, x, adj, alpha, rezero_w, out):
                 out=result[:],
                 in0=products[r, b][:],
                 scalar=alpha_f32[:, 0:1],
-                in1=x_rows[r][:, b % 2, b // 2, :],
+                in1=x_rows[r][:, place(b), :],
                 op0=MULT,
                 op1=ADD,
             )
             nc.sync.dma_start(out=out[first : first + P, :], in_=result[:])
 
-        squares = [
-            (g, diagonal - g)
-            for diagonal in range(2 * GROUPS - 1)
-            for g in range(max(0, diagonal - GROUPS + 1), diagonal // 2 + 1)
-        ]
-        grouped = {}
-        for n in range(len(squares) + 1 + LAG):
-            if n < len(squares):
-                grouped[n] = normalise_square(*squares[n])
-            if 0 < n <= len(squares):
-                quantise_square(*squares[n - 1], *grouped[n - 1])
-            if n > LAG:
-                r, last = squares[n - 1 - LAG]
-                if last == GROUPS - 1:
-                    for b in range(PACK):
-                        second_matmul(r, b)
-                        add_residual(r, b)
+        nc.scalar.copy(out=alpha_f32[:], in_=alpha_bf[:])
+        for s in range(GROUPS):
+            for q in range(GROUPS):
+                degree_sums(s, q)
+            degrees(s)
+        for h in range(GROUPS + 1):
+            regroup_half(h, 0)
+            regroup_half(h, 1)
+            (quantise_x(h) if h < GROUPS else quantise_w())
+        normalise(0, 0)
+        normalise(0, 1)
+        quantise_mirror(0, 0, 0, 4)
+        normalise(1, 1)
+        quantise_mirror(0, 1, 0, 4)
+        normalise(0, 2)
+        quantise_mirror(1, 1, 0, 4)
+        regroup_direct(0, 1)
+        quantise_direct(0, 1)
+        normalise(0, 3)
+        quantise_mirror(0, 2, 0, 4)
+        normalise(1, 2)
+        quantise_mirror(0, 3, 0, 1)
+        aggregate(0, 0)
+        quantise_agg(0, 0)
+        quantise_mirror(0, 3, 1, 1)
+        aggregate(0, 1)
+        quantise_agg(0, 1)
+        quantise_mirror(0, 3, 2, 1)
+        aggregate(0, 2)
+        quantise_agg(0, 2)
+        quantise_mirror(0, 3, 3, 1)
+        aggregate(0, 3)
+        quantise_agg(0, 3)
+        normalise(1, 3)
+        quantise_mirror(1, 2, 0, 4)
+        normalise(2, 2)
+        quantise_mirror(1, 3, 0, 1)
+        aggregate(1, 0)
+        quantise_agg(1, 0)
+        quantise_mirror(1, 3, 1, 1)
+        aggregate(1, 1)
+        quantise_agg(1, 1)
+        quantise_mirror(1, 3, 2, 1)
+        aggregate(1, 2)
+        quantise_agg(1, 2)
+        quantise_mirror(1, 3, 3, 1)
+        aggregate(1, 3)
+        quantise_agg(1, 3)
+        regroup_direct(0, 2)
+        quantise_direct(0, 2)
+        regroup_direct(1, 2)
+        quantise_direct(1, 2)
+        normalise(2, 3)
+        quantise_mirror(2, 2, 0, 4)
+        second_matmul(0, 0)
+        add_residual(0, 0)
+        second_matmul(0, 1)
+        add_residual(0, 1)
+        second_matmul(0, 2)
+        add_residual(0, 2)
+        second_matmul(0, 3)
+        add_residual(0, 3)
+        normalise(3, 3)
+        quantise_mirror(2, 3, 0, 1)
+        aggregate(2, 0)
+        quantise_agg(2, 0)
+        quantise_mirror(2, 3, 1, 1)
+        aggregate(2, 1)
+        quantise_agg(2, 1)
+        quantise_mirror(2, 3, 2, 1)
+        aggregate(2, 2)
+        quantise_agg(2, 2)
+        quantise_mirror(2, 3, 3, 1)
+        aggregate(2, 3)
+        quantise_agg(2, 3)
+        second_matmul(1, 0)
+        add_residual(1, 0)
+        second_matmul(1, 1)
+        add_residual(1, 1)
+        second_matmul(1, 2)
+        add_residual(1, 2)
+        second_matmul(1, 3)
+        add_residual(1, 3)
+        regroup_direct(0, 3)
+        quantise_direct(0, 3)
+        regroup_direct(1, 3)
+        quantise_direct(1, 3)
+        regroup_direct(2, 3)
+        quantise_direct(2, 3)
+        quantise_mirror(3, 3, 0, 1)
+        aggregate(3, 0)
+        quantise_agg(3, 0)
+        quantise_mirror(3, 3, 1, 1)
+        aggregate(3, 1)
+        quantise_agg(3, 1)
+        quantise_mirror(3, 3, 2, 1)
+        aggregate(3, 2)
+        quantise_agg(3, 2)
+        quantise_mirror(3, 3, 3, 1)
+        aggregate(3, 3)
+        quantise_agg(3, 3)
+        second_matmul(2, 0)
+        add_residual(2, 0)
+        second_matmul(2, 1)
+        add_residual(2, 1)
+        second_matmul(2, 2)
+        add_residual(2, 2)
+        second_matmul(2, 3)
+        add_residual(2, 3)
+        second_matmul(3, 0)
+        add_residual(3, 0)
+        second_matmul(3, 1)
+        add_residual(3, 1)
+        second_matmul(3, 2)
+        add_residual(3, 2)
+        second_matmul(3, 3)
+        add_residual(3, 3)

@@ -11,6 +11,7 @@ FP8X4 = mybir.dt.float8_e4m3fn_x4
 MULT = mybir.AluOpType.mult
 ADD = mybir.AluOpType.add
 SQRT = mybir.ActivationFunctionType.Sqrt
+COPY = mybir.ActivationFunctionType.Copy
 
 P = 128
 PACK = 4
@@ -18,9 +19,8 @@ GROUP = P * PACK
 NODES = 2048
 FEATURES = 512
 GROUPS = NODES // GROUP
-ONES_WIDTH = 32
-X_AFTER = {1: (0, 1), 2: (2, 3)}
-W_AFTER = 2
+X_BEFORE = ((), (), (0,), (1,))
+ONES_WIDTH = 48
 
 FLOPS = 2 * NODES * NODES * FEATURES + 2 * NODES * FEATURES * FEATURES
 
@@ -50,35 +50,37 @@ def tile_sage_re_pa_kernel(tc, x, adj, alpha, rezero_w, out):
         keep = pools.enter_context(tc.tile_pool(name="keep", bufs=1))
         stage = pools.enter_context(tc.tile_pool(name="stage", bufs=3))
         x_stage = pools.enter_context(tc.tile_pool(name="x_stage", bufs=2))
-        square_pool = pools.enter_context(tc.tile_pool(name="square_pool", bufs=8))
+        junk_pool = pools.enter_context(tc.tile_pool(name="junk_pool", bufs=2))
+        direct_pool = pools.enter_context(tc.tile_pool(name="direct_pool", bufs=3))
+        square_pool = pools.enter_context(tc.tile_pool(name="square_pool", bufs=7))
         rows_pool = pools.enter_context(tc.tile_pool(name="rows_pool", bufs=6))
         agg_pool = pools.enter_context(tc.tile_pool(name="agg_pool", bufs=1))
-        psum_sums = pools.enter_context(tc.psum_pool(name="psum_sums", bufs=1))
-        psum_wide = pools.enter_context(tc.psum_pool(name="psum_wide", bufs=3))
+        psum_wide = pools.enter_context(tc.psum_pool(name="psum_wide", bufs=4))
         psum_work = pools.enter_context(tc.psum_pool(name="psum_work", bufs=4))
 
         x_view = x.rearrange("(h e v p) c -> h v p e c", e=2, v=2, p=P)
-        adj_cols = []
+        adj_rows = []
         x_rows = []
+        for g in range(GROUPS):
+            for h in X_BEFORE[g]:
+                x_h = keep.tile([P, PACK, FEATURES], BF16, name="x_rows%d" % h)
+                for v in range(2):
+                    nc.sync.dma_start(out=x_h[:, 2 * v : 2 * v + 2, :], in_=x_view[h, v])
+                x_rows.append(x_h)
+            blocks = []
+            for t in range(PACK):
+                first = g * GROUP + t * P
+                block = keep.tile([P, NODES - g * GROUP], BF16, name="adj_%d_%d" % (g, t))
+                nc.sync.dma_start(out=block[:], in_=adj[first : first + P, g * GROUP :])
+                blocks.append(block)
+            adj_rows.append(blocks)
+        for h in range(len(x_rows), GROUPS):
+            x_h = keep.tile([P, PACK, FEATURES], BF16, name="x_rows%d" % h)
+            for v in range(2):
+                nc.sync.dma_start(out=x_h[:, 2 * v : 2 * v + 2, :], in_=x_view[h, v])
+            x_rows.append(x_h)
         w_rows = keep.tile([P, PACK, FEATURES], BF16)
-        for s in range(GROUPS):
-            adj_view = adj[:, s * GROUP : (s + 1) * GROUP].rearrange("(a p) f -> p a f", p=P)
-            pieces = []
-            for q in range(GROUPS):
-                piece = keep.tile([P, PACK, GROUP], BF16, name="adj_%d_%d" % (q, s))
-                nc.sync.dma_start(out=piece[:], in_=adj_view[:, q * PACK : (q + 1) * PACK, :])
-                pieces.append(piece)
-            adj_cols.append(pieces)
-            if s in X_AFTER:
-                for h in X_AFTER[s]:
-                    x_h = keep.tile([P, PACK, FEATURES], BF16, name="x_rows%d" % h)
-                    for v in range(2):
-                        nc.sync.dma_start(out=x_h[:, 2 * v : 2 * v + 2, :], in_=x_view[h, v])
-                    x_rows.append(x_h)
-            if s == W_AFTER:
-                nc.sync.dma_start(
-                    out=w_rows[:], in_=rezero_w.rearrange("(t p) n -> p t n", p=P)
-                )
+        nc.sync.dma_start(out=w_rows[:], in_=rezero_w.rearrange("(t p) n -> p t n", p=P))
         alpha_bf = keep.tile([P, 1], BF16)
         nc.scalar.dma_start(out=alpha_bf[:], in_=alpha.partition_broadcast(P))
 
@@ -92,29 +94,51 @@ def tile_sage_re_pa_kernel(tc, x, adj, alpha, rezero_w, out):
 
         dis_col = []
         dis_row = []
-        parts = {}
+        sums = psum_work.tile([P, GROUPS, GROUPS * PACK + ONES_WIDTH], F32, tag="work")
+        row_sums = [keep.tile([P, PACK], F32, name="row_sums%d" % g) for g in range(GROUPS - 1)]
 
-        def degree_sums(s, q):
-            if q == 0:
-                parts[s] = psum_sums.tile([P, GROUPS, PACK, ONES_WIDTH], F32, tag="sums", name="part")
+        def column_sums(q, g):
             for b in range(PACK):
+                first = (g - q) * GROUP + b * P
                 for t in range(PACK):
                     nc.tensor.matmul(
-                        out=parts[s][:, q, b, :],
-                        lhsT=adj_cols[s][q][:, t, b * P : (b + 1) * P],
+                        out=sums[:, g, q * PACK + b : q * PACK + b + ONES_WIDTH],
+                        lhsT=adj_rows[q][t][:, first : first + P],
                         rhs=ones[:],
                         start=(t == 0),
                         stop=(t == PACK - 1),
                     )
 
+        def sum_rows(g, t, on_scalar):
+            right = adj_rows[g][t][:, GROUP:]
+            copied = junk_pool.tile([P, NODES - (g + 1) * GROUP], BF16, name="copied")
+            if on_scalar:
+                nc.scalar.activation(
+                    out=copied[:], in_=right, func=COPY, accum_out=row_sums[g][:, t : t + 1]
+                )
+            else:
+                nc.vector.tensor_scalar(
+                    out=copied[:],
+                    in0=right,
+                    scalar1=1.0,
+                    scalar2=0.0,
+                    op0=MULT,
+                    op1=ADD,
+                    accum_out=row_sums[g][:, t : t + 1],
+                )
+
         def degrees(s):
             deg = stage.tile([P, PACK], F32)
             nc.vector.tensor_reduce(
                 out=deg[:],
-                in_=parts[s][:, :, :, 0].rearrange("p q b -> p b q"),
+                in_=sums[:, s, 0 : (s + 1) * PACK].rearrange("p (q b) -> p b q", b=PACK),
                 axis=mybir.AxisListType.X,
                 op=ADD,
             )
+            if s < GROUPS - 1:
+                below = deg
+                deg = stage.tile([P, PACK], F32, name="whole_deg")
+                nc.vector.tensor_tensor(out=deg[:], in0=below[:], in1=row_sums[s][:], op=ADD)
             inverse = stage.tile([P, PACK], F32)
             nc.vector.reciprocal(out=inverse[:], in_=deg[:])
             col_s = keep.tile([P, PACK], F32, name="dis_col%d" % s)
@@ -177,7 +201,9 @@ def tile_sage_re_pa_kernel(tc, x, adj, alpha, rezero_w, out):
             for t in range(PACK):
                 nc.vector.scalar_tensor_tensor(
                     out=square[:, place(t)],
-                    in0=adj_cols[s][g][:, t, :].rearrange("p (e w) -> p w e", e=2),
+                    in0=adj_rows[g][t][:, (s - g) * GROUP : (s - g + 1) * GROUP].rearrange(
+                        "p (e w) -> p w e", e=2
+                    ),
                     scalar=dis_col[g][:, t : t + 1],
                     in1=dis_row[s][:],
                     op0=MULT,
@@ -198,13 +224,13 @@ def tile_sage_re_pa_kernel(tc, x, adj, alpha, rezero_w, out):
             squares[g, s] = square
             mirrors[g, s] = mirrored
 
-        def regroup_direct(g, s, engine_copy=nc.scalar.copy):
+        def regroup_direct(g, s, halves=range(2), engine_copy=nc.scalar.copy):
             square = squares[g, s]
-            direct = stage.tile([P, GROUP, PACK], BF16, align_bytes=64)
-            for half in range(2):
+            if (g, s) not in directs:
+                directs[g, s] = direct_pool.tile([P, GROUP, PACK], BF16, align_bytes=64, name="direct")
+            for half in halves:
                 cols = slice(half * 2 * P, (half + 1) * 2 * P)
-                regroup(engine_copy, direct[:, cols, :], square[:, :, :, half])
-            directs[g, s] = direct
+                regroup(engine_copy, directs[g, s][:, cols, :], square[:, :, :, half])
 
         def quantise_direct(g, s):
             quantise(nc, directs[g, s], n_codes[g, s][:], n_scales[g, s][:])
@@ -273,10 +299,32 @@ def tile_sage_re_pa_kernel(tc, x, adj, alpha, rezero_w, out):
             nc.sync.dma_start(out=out[first : first + P, :], in_=result[:])
 
         nc.scalar.copy(out=alpha_f32[:], in_=alpha_bf[:])
-        for s in range(GROUPS):
-            for q in range(GROUPS):
-                degree_sums(s, q)
-            degrees(s)
+        sum_rows(0, 0, on_scalar=False)
+        sum_rows(0, 1, on_scalar=True)
+        sum_rows(0, 2, on_scalar=False)
+        sum_rows(0, 3, on_scalar=True)
+        column_sums(0, 0)
+        degrees(0)
+        sum_rows(1, 0, on_scalar=False)
+        sum_rows(1, 1, on_scalar=False)
+        sum_rows(1, 2, on_scalar=False)
+        sum_rows(1, 3, on_scalar=False)
+        column_sums(0, 1)
+        column_sums(1, 1)
+        degrees(1)
+        sum_rows(2, 0, on_scalar=False)
+        sum_rows(2, 1, on_scalar=False)
+        sum_rows(2, 2, on_scalar=False)
+        sum_rows(2, 3, on_scalar=False)
+        column_sums(0, 2)
+        column_sums(1, 2)
+        column_sums(2, 2)
+        degrees(2)
+        column_sums(0, 3)
+        column_sums(1, 3)
+        column_sums(2, 3)
+        column_sums(3, 3)
+        degrees(3)
         for h in range(GROUPS + 1):
             regroup_half(h, 0)
             regroup_half(h, 1)
@@ -284,15 +332,11 @@ def tile_sage_re_pa_kernel(tc, x, adj, alpha, rezero_w, out):
         normalise(0, 0)
         normalise(0, 1)
         quantise_mirror(0, 0, 0, 4)
-        normalise(1, 1)
-        quantise_mirror(0, 1, 0, 4)
         normalise(0, 2)
-        quantise_mirror(1, 1, 0, 4)
-        regroup_direct(0, 1)
-        quantise_direct(0, 1)
+        quantise_mirror(0, 1, 0, 4)
         normalise(0, 3)
         quantise_mirror(0, 2, 0, 4)
-        normalise(1, 2)
+        normalise(1, 1)
         quantise_mirror(0, 3, 0, 1)
         aggregate(0, 0)
         quantise_agg(0, 0)
@@ -305,6 +349,10 @@ def tile_sage_re_pa_kernel(tc, x, adj, alpha, rezero_w, out):
         quantise_mirror(0, 3, 3, 1)
         aggregate(0, 3)
         quantise_agg(0, 3)
+        normalise(1, 2)
+        quantise_mirror(1, 1, 0, 4)
+        regroup_direct(0, 1)
+        quantise_direct(0, 1)
         normalise(1, 3)
         quantise_mirror(1, 2, 0, 4)
         normalise(2, 2)
@@ -320,12 +368,6 @@ def tile_sage_re_pa_kernel(tc, x, adj, alpha, rezero_w, out):
         quantise_mirror(1, 3, 3, 1)
         aggregate(1, 3)
         quantise_agg(1, 3)
-        regroup_direct(0, 2)
-        quantise_direct(0, 2)
-        regroup_direct(1, 2)
-        quantise_direct(1, 2)
-        normalise(2, 3)
-        quantise_mirror(2, 2, 0, 4)
         second_matmul(0, 0)
         add_residual(0, 0)
         second_matmul(0, 1)
@@ -334,6 +376,12 @@ def tile_sage_re_pa_kernel(tc, x, adj, alpha, rezero_w, out):
         add_residual(0, 2)
         second_matmul(0, 3)
         add_residual(0, 3)
+        regroup_direct(0, 2)
+        quantise_direct(0, 2)
+        regroup_direct(1, 2)
+        quantise_direct(1, 2)
+        normalise(2, 3)
+        quantise_mirror(2, 2, 0, 4)
         normalise(3, 3)
         quantise_mirror(2, 3, 0, 1)
         aggregate(2, 0)

@@ -198,28 +198,32 @@ def tile_sage_re_pa_kernel(tc, x, adj, alpha, rezero_w, out):
                 .bitcast(F32)
                 .rearrange("p (c v) -> p c v", v=2)
             )
-            for t in range(PACK):
-                nc.vector.scalar_tensor_tensor(
-                    out=square[:, place(t)],
-                    in0=adj_rows[g][t][:, (s - g) * GROUP : (s - g + 1) * GROUP].rearrange(
-                        "p (e w) -> p w e", e=2
-                    ),
-                    scalar=dis_col[g][:, t : t + 1],
-                    in1=dis_row[s][:],
-                    op0=MULT,
-                    op1=MULT,
-                )
-                words = square[:, place(t)].rearrange("p w e -> p (w e)").bitcast(F32)
-                flipped = psum_work.tile([P, 2, P], F32, tag="work")
-                for v in range(2):
-                    nc.tensor.transpose(
-                        out=flipped[:, v, :],
-                        in_=words[:, v * P : (v + 1) * P],
-                        identity=ident_f32[:],
+            for pair in range(2):
+                flipped = psum_work.tile([P, 2, 2, P], F32, tag="work")
+                for t in range(2):
+                    block = 2 * pair + t
+                    nc.vector.scalar_tensor_tensor(
+                        out=square[:, place(block)],
+                        in0=adj_rows[g][block][:, (s - g) * GROUP : (s - g + 1) * GROUP].rearrange(
+                            "p (e w) -> p w e", e=2
+                        ),
+                        scalar=dis_col[g][:, block : block + 1],
+                        in1=dis_row[s][:],
+                        op0=MULT,
+                        op1=MULT,
                     )
+                    words = square[:, place(block)].rearrange("p w e -> p (w e)").bitcast(F32)
+                    for v in range(2):
+                        nc.tensor.transpose(
+                            out=flipped[:, t, v, :],
+                            in_=words[:, v * P : (v + 1) * P],
+                            identity=ident_f32[:],
+                        )
                 nc.scalar.copy(
-                    out=mirrored_words[:, t * P : (t + 1) * P, :],
-                    in_=flipped.rearrange("p v i -> p i v"),
+                    out=mirrored_words[:, 2 * pair * P : 2 * (pair + 1) * P, :].rearrange(
+                        "p (t i) v -> p t i v", t=2
+                    ),
+                    in_=flipped.rearrange("p t v i -> p t i v"),
                 )
             squares[g, s] = square
             mirrors[g, s] = mirrored
@@ -300,15 +304,15 @@ def tile_sage_re_pa_kernel(tc, x, adj, alpha, rezero_w, out):
 
         nc.scalar.copy(out=alpha_f32[:], in_=alpha_bf[:])
         sum_rows(0, 0, on_scalar=False)
-        sum_rows(0, 1, on_scalar=True)
+        sum_rows(0, 1, on_scalar=False)
         sum_rows(0, 2, on_scalar=False)
-        sum_rows(0, 3, on_scalar=True)
+        sum_rows(0, 3, on_scalar=False)
         column_sums(0, 0)
         degrees(0)
-        sum_rows(1, 0, on_scalar=False)
-        sum_rows(1, 1, on_scalar=False)
-        sum_rows(1, 2, on_scalar=False)
-        sum_rows(1, 3, on_scalar=False)
+        sum_rows(1, 0, on_scalar=True)
+        sum_rows(1, 1, on_scalar=True)
+        sum_rows(1, 2, on_scalar=True)
+        sum_rows(1, 3, on_scalar=True)
         column_sums(0, 1)
         column_sums(1, 1)
         degrees(1)
@@ -337,16 +341,13 @@ def tile_sage_re_pa_kernel(tc, x, adj, alpha, rezero_w, out):
         normalise(0, 3)
         quantise_mirror(0, 2, 0, 4)
         normalise(1, 1)
-        quantise_mirror(0, 3, 0, 1)
+        quantise_mirror(0, 3, 0, 4)
         aggregate(0, 0)
         quantise_agg(0, 0)
-        quantise_mirror(0, 3, 1, 1)
         aggregate(0, 1)
         quantise_agg(0, 1)
-        quantise_mirror(0, 3, 2, 1)
         aggregate(0, 2)
         quantise_agg(0, 2)
-        quantise_mirror(0, 3, 3, 1)
         aggregate(0, 3)
         quantise_agg(0, 3)
         normalise(1, 2)
@@ -356,16 +357,13 @@ def tile_sage_re_pa_kernel(tc, x, adj, alpha, rezero_w, out):
         normalise(1, 3)
         quantise_mirror(1, 2, 0, 4)
         normalise(2, 2)
-        quantise_mirror(1, 3, 0, 1)
+        quantise_mirror(1, 3, 0, 4)
         aggregate(1, 0)
         quantise_agg(1, 0)
-        quantise_mirror(1, 3, 1, 1)
         aggregate(1, 1)
         quantise_agg(1, 1)
-        quantise_mirror(1, 3, 2, 1)
         aggregate(1, 2)
         quantise_agg(1, 2)
-        quantise_mirror(1, 3, 3, 1)
         aggregate(1, 3)
         quantise_agg(1, 3)
         second_matmul(0, 0)
@@ -383,16 +381,13 @@ def tile_sage_re_pa_kernel(tc, x, adj, alpha, rezero_w, out):
         normalise(2, 3)
         quantise_mirror(2, 2, 0, 4)
         normalise(3, 3)
-        quantise_mirror(2, 3, 0, 1)
+        quantise_mirror(2, 3, 0, 4)
         aggregate(2, 0)
         quantise_agg(2, 0)
-        quantise_mirror(2, 3, 1, 1)
         aggregate(2, 1)
         quantise_agg(2, 1)
-        quantise_mirror(2, 3, 2, 1)
         aggregate(2, 2)
         quantise_agg(2, 2)
-        quantise_mirror(2, 3, 3, 1)
         aggregate(2, 3)
         quantise_agg(2, 3)
         second_matmul(1, 0)
@@ -405,20 +400,17 @@ def tile_sage_re_pa_kernel(tc, x, adj, alpha, rezero_w, out):
         add_residual(1, 3)
         regroup_direct(0, 3)
         quantise_direct(0, 3)
-        regroup_direct(1, 3)
+        regroup_direct(1, 3, engine_copy=nc.vector.tensor_copy)
         quantise_direct(1, 3)
-        regroup_direct(2, 3)
+        regroup_direct(2, 3, engine_copy=nc.vector.tensor_copy)
         quantise_direct(2, 3)
-        quantise_mirror(3, 3, 0, 1)
+        quantise_mirror(3, 3, 0, 4)
         aggregate(3, 0)
         quantise_agg(3, 0)
-        quantise_mirror(3, 3, 1, 1)
         aggregate(3, 1)
         quantise_agg(3, 1)
-        quantise_mirror(3, 3, 2, 1)
         aggregate(3, 2)
         quantise_agg(3, 2)
-        quantise_mirror(3, 3, 3, 1)
         aggregate(3, 3)
         quantise_agg(3, 3)
         second_matmul(2, 0)

from contextlib import ExitStack

import concourse.mybir as mybir
from concourse.masks import make_identity

BF16 = mybir.dt.bfloat16
F32 = mybir.dt.float32
U32 = mybir.dt.uint32
U8 = mybir.dt.uint8
FP8X4 = mybir.dt.float8_e4m3fn_x4
MULT = mybir.AluOpType.mult
ADD = mybir.AluOpType.add
SQRT = mybir.ActivationFunctionType.Sqrt
COPY = mybir.ActivationFunctionType.Copy

P = 128
PACK = 4
GROUP = P * PACK
NODES = 2048
FEATURES = 512
GROUPS = NODES // GROUP
X_BEFORE = ((), (), (0,), (1,))
ONES_WIDTH = 48

FLOPS = 2 * NODES * NODES * FEATURES + 2 * NODES * FEATURES * FEATURES


def regroup(engine_copy, grouped, planes):
    engine_copy(
        out=grouped.rearrange("p (c i) t -> p c t i", i=4),
        in_=planes.rearrange("p t (c i) -> p c t i", i=4),
    )


def place(t):
    return 2 * (t % 2) + t // 2


def quantise(nc, grouped, codes, scales):
    nc.vector.quantize_mx(
        out=codes.bitcast(FP8X4),
        scales=scales,
        in_=grouped.rearrange("p c t -> p (c t)"),
    )


def tile_sage_re_pa_kernel(tc, x, adj, alpha, rezero_w, out):
    nc = tc.nc
    with ExitStack() as pools:
        keep = pools.enter_context(tc.tile_pool(name="keep", bufs=1))
        stage = pools.enter_context(tc.tile_pool(name="stage", bufs=3))
        x_stage = pools.enter_context(tc.tile_pool(name="x_stage", bufs=2))
        junk_pool = pools.enter_context(tc.tile_pool(name="junk_pool", bufs=2))
        direct_pool = pools.enter_context(tc.tile_pool(name="direct_pool", bufs=3))
        square_pool = pools.enter_context(tc.tile_pool(name="square_pool", bufs=7))
        rows_pool = pools.enter_context(tc.tile_pool(name="rows_pool", bufs=6))
        agg_pool = pools.enter_context(tc.tile_pool(name="agg_pool", bufs=1))
        psum_wide = pools.enter_context(tc.psum_pool(name="psum_wide", bufs=4))
        psum_work = pools.enter_context(tc.psum_pool(name="psum_work", bufs=4))

        x_view = x.rearrange("(h e v p) c -> h v p e c", e=2, v=2, p=P)
        adj_rows = []
        x_rows = []
        for g in range(GROUPS):
            for h in X_BEFORE[g]:
                x_h = keep.tile([P, PACK, FEATURES], BF16, name="x_rows%d" % h)
                for v in range(2):
                    nc.sync.dma_start(out=x_h[:, 2 * v : 2 * v + 2, :], in_=x_view[h, v])
                x_rows.append(x_h)
            blocks = []
            for t in range(PACK):
                first = g * GROUP + t * P
                block = keep.tile([P, NODES - g * GROUP], BF16, name="adj_%d_%d" % (g, t))
                nc.sync.dma_start(out=block[:], in_=adj[first : first + P, g * GROUP :])
                blocks.append(block)
            adj_rows.append(blocks)
        for h in range(len(x_rows), GROUPS):
            x_h = keep.tile([P, PACK, FEATURES], BF16, name="x_rows%d" % h)
            for v in range(2):
                nc.sync.dma_start(out=x_h[:, 2 * v : 2 * v + 2, :], in_=x_view[h, v])
            x_rows.append(x_h)
        w_rows = keep.tile([P, PACK, FEATURES], BF16)
        nc.sync.dma_start(out=w_rows[:], in_=rezero_w.rearrange("(t p) n -> p t n", p=P))
        alpha_bf = keep.tile([P, 1], BF16)
        nc.scalar.dma_start(out=alpha_bf[:], in_=alpha.partition_broadcast(P))

        ones = keep.tile([P, ONES_WIDTH], BF16)
        nc.vector.memset(ones[:], 1.0)
        ident_f32 = keep.tile([P, P], F32)
        make_identity(nc, ident_f32[:])
        alpha_f32 = keep.tile([P, 1], F32)
        warm = keep.tile([P, 1], F32)
        nc.scalar.activation(out=warm[:], in_=ones[:, 0:1], func=SQRT)

        dis_col = []
        dis_row = []
        sums = psum_work.tile([P, GROUPS, GROUPS * PACK + ONES_WIDTH], F32, tag="work")
        row_sums = [keep.tile([P, PACK], F32, name="row_sums%d" % g) for g in range(GROUPS - 1)]

        def column_sums(q, g):
            for b in range(PACK):
                first = (g - q) * GROUP + b * P
                for t in range(PACK):
                    nc.tensor.matmul(
                        out=sums[:, g, q * PACK + b : q * PACK + b + ONES_WIDTH],
                        lhsT=adj_rows[q][t][:, first : first + P],
                        rhs=ones[:],
                        start=(t == 0),
                        stop=(t == PACK - 1),
                    )

        def sum_rows(g, t, on_scalar):
            right = adj_rows[g][t][:, GROUP:]
            copied = junk_pool.tile([P, NODES - (g + 1) * GROUP], BF16, name="copied")
            if on_scalar:
                nc.scalar.activation(
                    out=copied[:], in_=right, func=COPY, accum_out=row_sums[g][:, t : t + 1]
                )
            else:
                nc.vector.tensor_scalar(
                    out=copied[:],
                    in0=right,
                    scalar1=1.0,
                    scalar2=0.0,
                    op0=MULT,
                    op1=ADD,
                    accum_out=row_sums[g][:, t : t + 1],
                )

        def degrees(s):
            deg = stage.tile([P, PACK], F32)
            nc.vector.tensor_reduce(
                out=deg[:],
                in_=sums[:, s, 0 : (s + 1) * PACK].rearrange("p (q b) -> p b q", b=PACK),
                axis=mybir.AxisListType.X,
                op=ADD,
            )
            if s < GROUPS - 1:
                below = deg
                deg = stage.tile([P, PACK], F32, name="whole_deg")
                nc.vector.tensor_tensor(out=deg[:], in0=below[:], in1=row_sums[s][:], op=ADD)
            inverse = stage.tile([P, PACK], F32)
            nc.vector.reciprocal(out=inverse[:], in_=deg[:])
            col_s = keep.tile([P, PACK], F32, name="dis_col%d" % s)
            nc.scalar.activation(out=col_s[:], in_=inverse[:], func=SQRT)
            dis_col.append(col_s)
            row_s = psum_wide.tile([P, 2 * P, 2], F32, tag="wide")
            for b in range(PACK):
                nc.tensor.transpose(
                    out=row_s[:, b % 2 * P : (b % 2 + 1) * P, b // 2],
                    in_=col_s[:, b : b + 1].to_broadcast([P, P]),
                    identity=ident_f32[:],
                )
            dis_row.append(row_s)

        x_codes = []
        x_scales = []
        for h in range(GROUPS):
            x_codes.append(keep.tile([P, FEATURES], U32, name="x_codes%d" % h, align_bytes=64))
            x_scales.append(keep.tile([P, FEATURES], U8, name="x_scales%d" % h, align_bytes=64))
        w_codes = keep.tile([P, FEATURES], U32, align_bytes=64)
        w_scales = keep.tile([P, FEATURES], U8, align_bytes=64)
        x_grouped = {}

        def regroup_half(h, half):
            if half == 0:
                x_grouped[h] = x_stage.tile([P, FEATURES, PACK], BF16, align_bytes=64, name="x_grouped")
            cols = slice(half * FEATURES // 2, (half + 1) * FEATURES // 2)
            planes = x_rows[h] if h < GROUPS else w_rows
            regroup(nc.scalar.copy, x_grouped[h][:, cols, :], planes[:, :, cols])

        def quantise_x(h):
            quantise(nc, x_grouped[h], x_codes[h][:], x_scales[h][:])

        def quantise_w():
            quantise(nc, x_grouped[GROUPS], w_codes[:], w_scales[:])

        n_codes = {}
        n_scales = {}
        for h in range(GROUPS):
            for r in range(GROUPS):
                n_codes[h, r] = keep.tile(
                    [P, GROUP], U32, name="n_codes_%d_%d" % (h, r), align_bytes=64
                )
                n_scales[h, r] = keep.tile(
                    [P, GROUP], U8, name="n_scales_%d_%d" % (h, r), align_bytes=64
                )

        squares = {}
        mirrors = {}
        directs = {}

        def normalise(g, s):
            square = square_pool.tile([P, PACK, 2 * P, 2], BF16)
            mirrored = stage.tile([P, GROUP, PACK], BF16, align_bytes=64)
            mirrored_words = (
                mirrored.rearrange("p c t -> p (c t)")
                .bitcast(F32)
                .rearrange("p (c v) -> p c v", v=2)
            )
            for pair in range(2):
                flipped = psum_work.tile([P, 2, 2, P], F32, tag="work")
                for t in range(2):
                    block = 2 * pair + t
                    nc.vector.scalar_tensor_tensor(
                        out=square[:, place(block)],
                        in0=adj_rows[g][block][:, (s - g) * GROUP : (s - g + 1) * GROUP].rearrange(
                            "p (e w) -> p w e", e=2
                        ),
                        scalar=dis_col[g][:, block : block + 1],
                        in1=dis_row[s][:],
                        op0=MULT,
                        op1=MULT,
                    )
                    words = square[:, place(block)].rearrange("p w e -> p (w e)").bitcast(F32)
                    for v in range(2):
                        nc.tensor.transpose(
                            out=flipped[:, t, v, :],
                            in_=words[:, v * P : (v + 1) * P],
                            identity=ident_f32[:],
                        )
                nc.scalar.copy(
                    out=mirrored_words[:, 2 * pair * P : 2 * (pair + 1) * P, :].rearrange(
                        "p (t i) v -> p t i v", t=2
                    ),
                    in_=flipped.rearrange("p t v i -> p t i v"),
                )
            squares[g, s] = square
            mirrors[g, s] = mirrored

        def regroup_direct(g, s, halves=range(2), engine_copy=nc.scalar.copy):
            square = squares[g, s]
            if (g, s) not in directs:
                directs[g, s] = direct_pool.tile([P, GROUP, PACK], BF16, align_bytes=64, name="direct")
            for half in halves:
                cols = slice(half * 2 * P, (half + 1) * 2 * P)
                regroup(engine_copy, directs[g, s][:, cols, :], square[:, :, :, half])

        def quantise_direct(g, s):
            quantise(nc, directs[g, s], n_codes[g, s][:], n_scales[g, s][:])

        def quantise_mirror(g, s, first, count):
            cols = slice(first * P, (first + count) * P)
            quantise(nc, mirrors[g, s][:, cols, :], n_codes[s, g][:, cols], n_scales[s, g][:, cols])

        agg_codes = {}
        agg_scales = {}
        agg_grouped = {}

        def aggregate(r, b):
            cols = slice(b * P, (b + 1) * P)
            agg_t = psum_work.tile([P, PACK, P], F32, tag="work")
            for t in range(PACK):
                for h in range(GROUPS):
                    nc.tensor.matmul_mx(
                        out=agg_t[:, t, :],
                        lhsT=x_codes[h][:, t * P : (t + 1) * P].bitcast(FP8X4),
                        lhsT_scale=x_scales[h][:, t * P : (t + 1) * P],
                        rhs=n_codes[h, r][:, cols].bitcast(FP8X4),
                        rhs_scale=n_scales[h, r][:, cols],
                        start=(h == 0),
                        stop=(h == GROUPS - 1),
                    )
            grouped = rows_pool.tile([P, P, PACK], BF16, align_bytes=64)
            nc.scalar.copy(out=grouped[:], in_=agg_t.rearrange("p t m -> p m t"))
            agg_grouped[r, b] = grouped

        def quantise_agg(r, b):
            agg_codes[r, b] = agg_pool.tile(
                [P, P], U32, name="agg_codes_%d_%d" % (r, b), align_bytes=64
            )
            agg_scales[r, b] = agg_pool.tile(
                [P, P], U8, name="agg_scales_%d_%d" % (r, b), align_bytes=64
            )
            quantise(nc, agg_grouped[r, b], agg_codes[r, b][:], agg_scales[r, b][:])

        products = {}

        def second_matmul(r, b):
            product = psum_wide.tile([P, FEATURES], F32, tag="wide")
            nc.tensor.matmul_mx(
                out=product[:],
                lhsT=agg_codes[r, b][:].bitcast(FP8X4),
                lhsT_scale=agg_scales[r, b][:],
                rhs=w_codes[:].bitcast(FP8X4),
                rhs_scale=w_scales[:],
                start=True,
                stop=True,
            )
            products[r, b] = product

        def add_residual(r, b):
            first = r * GROUP + b * P
            result = rows_pool.tile([P, FEATURES], F32)
            nc.vector.scalar_tensor_tensor(
                out=result[:],
                in0=products[r, b][:],
                scalar=alpha_f32[:, 0:1],
                in1=x_rows[r][:, place(b), :],
                op0=MULT,
                op1=ADD,
            )
            nc.sync.dma_start(out=out[first : first + P, :], in_=result[:])

        nc.scalar.copy(out=alpha_f32[:], in_=alpha_bf[:])
        sum_rows(0, 0, on_scalar=False)
        sum_rows(0, 1, on_scalar=False)
        sum_rows(0, 2, on_scalar=False)
        sum_rows(0, 3, on_scalar=False)
        column_sums(0, 0)
        degrees(0)
        sum_rows(1, 0, on_scalar=True)
        sum_rows(1, 1, on_scalar=True)
        sum_rows(1, 2, on_scalar=True)
        sum_rows(1, 3, on_scalar=True)
        column_sums(0, 1)
        column_sums(1, 1)
        degrees(1)
        sum_rows(2, 0, on_scalar=False)
        sum_rows(2, 1, on_scalar=False)
        sum_rows(2, 2, on_scalar=False)
        sum_rows(2, 3, on_scalar=False)
        column_sums(0, 2)
        column_sums(1, 2)
        column_sums(2, 2)
        degrees(2)
        column_sums(0, 3)
        column_sums(1, 3)
        column_sums(2, 3)
        column_sums(3, 3)
        degrees(3)
        for h in range(GROUPS + 1):
            regroup_half(h, 0)
            regroup_half(h, 1)
            (quantise_x(h) if h < GROUPS else quantise_w())
        normalise(0, 0)
        normalise(0, 1)
        quantise_mirror(0, 0, 0, 4)
        normalise(0, 2)
        quantise_mirror(0, 1, 0, 4)
        normalise(0, 3)
        quantise_mirror(0, 2, 0, 4)
        normalise(1, 1)
        quantise_mirror(0, 3, 0, 4)
        aggregate(0, 0)
        quantise_agg(0, 0)
        aggregate(0, 1)
        quantise_agg(0, 1)
        aggregate(0, 2)
        quantise_agg(0, 2)
        aggregate(0, 3)
        quantise_agg(0, 3)
        normalise(1, 2)
        quantise_mirror(1, 1, 0, 4)
        regroup_direct(0, 1)
        quantise_direct(0, 1)
        normalise(1, 3)
        quantise_mirror(1, 2, 0, 4)
        normalise(2, 2)
        quantise_mirror(1, 3, 0, 4)
        aggregate(1, 0)
        quantise_agg(1, 0)
        aggregate(1, 1)
        quantise_agg(1, 1)
        aggregate(1, 2)
        quantise_agg(1, 2)
        aggregate(1, 3)
        quantise_agg(1, 3)
        second_matmul(0, 0)
        add_residual(0, 0)
        second_matmul(0, 1)
        add_residual(0, 1)
        second_matmul(0, 2)
        add_residual(0, 2)
        second_matmul(0, 3)
        add_residual(0, 3)
        regroup_direct(0, 2)
        quantise_direct(0, 2)
        regroup_direct(1, 2)
        quantise_direct(1, 2)
        normalise(2, 3)
        quantise_mirror(2, 2, 0, 4)
        normalise(3, 3)
        quantise_mirror(2, 3, 0, 4)
        aggregate(2, 0)
        quantise_agg(2, 0)
        aggregate(2, 1)
        quantise_agg(2, 1)
        aggregate(2, 2)
        quantise_agg(2, 2)
        aggregate(2, 3)
        quantise_agg(2, 3)
        second_matmul(1, 0)
        add_residual(1, 0)
        second_matmul(1, 1)
        add_residual(1, 1)
        second_matmul(1, 2)
        add_residual(1, 2)
        second_matmul(1, 3)
        add_residual(1, 3)
        regroup_direct(0, 3)
        quantise_direct(0, 3)
        regroup_direct(1, 3, engine_copy=nc.vector.tensor_copy)
        quantise_direct(1, 3)
        regroup_direct(2, 3, engine_copy=nc.vector.tensor_copy)
        quantise_direct(2, 3)
        quantise_mirror(3, 3, 0, 4)
        aggregate(3, 0)
        quantise_agg(3, 0)
        aggregate(3, 1)
        quantise_agg(3, 1)
        aggregate(3, 2)
        quantise_agg(3, 2)
        aggregate(3, 3)
        quantise_agg(3, 3)
        second_matmul(2, 0)
        add_residual(2, 0)
        second_matmul(2, 1)
        add_residual(2, 1)
        second_matmul(2, 2)
        add_residual(2, 2)
        second_matmul(2, 3)
        add_residual(2, 3)
        second_matmul(3, 0)
        add_residual(3, 0)
        second_matmul(3, 1)
        add_residual(3, 1)
        second_matmul(3, 2)
        add_residual(3, 2)
        second_matmul(3, 3)
        add_residual(3, 3)
